import numpy as np
import ml_dtypes


def mxq(x, axis, fmt="e4m3"):
    dtype, down = {"e4m3": (ml_dtypes.float8_e4m3fn, 7), "e5m2": (ml_dtypes.float8_e5m2, 14)}[fmt]
    v = np.moveaxis(np.asarray(x, np.float32).astype(ml_dtypes.bfloat16).astype(np.float64), axis, -1)
    blocks = v.reshape(v.shape[:-1] + (-1, 32))
    amax = np.abs(blocks).max(-1, keepdims=True)
    byte = np.maximum(np.where(amax > 0, np.frexp(amax)[1] - 1 + 127, 0) - down, 1)
    scale = np.exp2(byte - 127.0)
    codes = (blocks / scale).astype(np.float32).astype(dtype).astype(np.float64)
    return np.moveaxis((codes * scale).reshape(v.shape), -1, axis)


WIDE = False


def mx_kscale(k):
    if not WIDE:
        return np.ones(k)
    levels = np.array([10, -10, 5, -5, 0])
    a = np.random.permutation(np.resize(levels, k // 512 * 4)).reshape(k // 512, 4)
    idx = np.arange(k)
    return np.exp2(a[idx // 512, idx % 128 // 32])


BF16 = ml_dtypes.bfloat16


def bf(x):
    return np.asarray(x, np.float32).astype(BF16)


def f64(x):
    return np.asarray(x).astype(np.float64)


B, S, E, H = 4, 1024, 512, 8
DH = E // H
EPS = 1e-5


def heads(t):
    return t.reshape(B, S, H, DH).transpose(0, 2, 1, 3)


def setup_inputs():
    s = mx_kscale(E)
    tok = np.exp2(np.random.uniform(-7.5, 1.5, (B, S, 1)))
    off = 0.5 * np.random.standard_normal((B, S, 1))
    return {"inputs": bf((np.random.standard_normal((B, S, E)) + off) * tok),
            "ln_w": bf((1.0 + 0.1 * np.random.standard_normal(E)) * s),
            "ln_b": bf(0.1 * np.random.standard_normal(E) * s),
            "w_qkv": bf(np.random.standard_normal((3 * E, E)) / np.sqrt(E) / s[None, :])}


def reference(inputs, ln_w, ln_b, w_qkv):
    a = f64(inputs)
    mu = a.mean(-1, keepdims=True)
    var = a.var(-1, keepdims=True)
    x = (a - mu) / np.sqrt(var + EPS) * f64(ln_w) + f64(ln_b)
    qkv = mxq(x, 2, "e4m3") @ mxq(f64(w_qkv), 1, "e4m3").T
    q, k, v = np.split(qkv, 3, axis=-1)
    return heads(q), heads(k), heads(v)

@@ -1,0 +1,260 @@
+from contextlib import ExitStack
+
+import concourse.mybir as mybir
+from concourse.masks import make_identity
+
+FLOPS = 2 * 4096 * 1536 * 512
+
+F32 = mybir.dt.float32
+BF16 = mybir.dt.bfloat16
+U32 = mybir.dt.uint32
+U8 = mybir.dt.uint8
+FP8X4 = mybir.dt.float8_e4m3fn_x4
+ALU = mybir.AluOpType
+ACT = mybir.ActivationFunctionType
+
+P = 128
+NB, SEQ, E, H, DH = 4, 1024, 512, 8, 64
+J = SEQ // P
+G = 4
+NG = NB * J // G
+EPS = 1e-5
+
+
+def tile_selfattention_pa_t_kernel(tc, inputs, ln_w, ln_b, w_qkv, out_0, out_1, out_2):
+    nc = tc.nc
+    outs = (out_0, out_1, out_2)
+    with ExitStack() as ctx:
+        keep = ctx.enter_context(tc.tile_pool(name="keep", bufs=1))
+        wgp = ctx.enter_context(tc.tile_pool(name="wgp", bufs=2))
+        sp = ctx.enter_context(tc.tile_pool(name="sp", bufs=4))
+        xnp = ctx.enter_context(tc.tile_pool(name="xnp", bufs=8))
+        plp = ctx.enter_context(tc.tile_pool(name="plp", bufs=2))
+        grp = ctx.enter_context(tc.tile_pool(name="grp", bufs=2))
+        osp = ctx.enter_context(tc.tile_pool(name="osp", bufs=6))
+        xtp = ctx.enter_context(tc.psum_pool(name="xtp", bufs=1))
+        accp = ctx.enter_context(tc.psum_pool(name="accp", bufs=4))
+
+        wb_raw = keep.tile([P, 2 * P], BF16, name="wb_raw")
+        nc.vector.memset(wb_raw[:], 0.0)
+        one_t = keep.tile([P, 1], F32, name="one_t")
+        nc.vector.memset(one_t[:], 1.0)
+        junk = keep.tile([P, 1], F32, name="junk")
+        nc.scalar.activation(out=junk[:], in_=one_t[:], func=ACT.Sqrt)
+        ident = keep.tile([P, P], F32, name="ident")
+        make_identity(nc, ident[:])
+
+        x_sb = [keep.tile([P, J, E], BF16, name="x%d" % b) for b in range(NB)]
+        w_sb = keep.tile([P, 12, E], BF16, name="w_sb")
+        xv = [inputs[b].rearrange("(p j) k -> p j k", j=J) for b in range(NB)]
+
+        def load_w(t):
+            nc.sync.dma_start(
+                out=w_sb[:, 4 * t : 4 * t + 4, :],
+                in_=w_qkv[512 * t : 512 * t + 512, :].rearrange("(r p) k -> p r k", p=P),
+            )
+
+        nc.sync.dma_start(out=x_sb[0][:, 0:4, :], in_=xv[0][:, 0:4, :])
+        nc.sync.dma_start(out=wb_raw[0:2, :], in_=ln_w.rearrange("(u c) -> u c", u=2))
+        nc.sync.dma_start(out=wb_raw[2:4, :], in_=ln_b.rearrange("(u c) -> u c", u=2))
+        load_w(0)
+        nc.sync.dma_start(out=x_sb[0][:, 4:8, :], in_=xv[0][:, 4:8, :])
+        load_w(1)
+        load_w(2)
+        for b in range(1, NB):
+            nc.sync.dma_start(out=x_sb[b][:], in_=xv[b])
+
+        wcodes = keep.tile([P, 1536], U32, name="wcodes", align_bytes=64)
+        wscales = keep.tile([P, 1536], U8, name="wscales", align_bytes=64)
+        xc = [keep.tile([P, 512], U32, name="xc%d" % g, align_bytes=64) for g in range(NG)]
+        xs = [keep.tile([P, 512], U8, name="xs%d" % g, align_bytes=64) for g in range(NG)]
+        wbc = keep.tile([P, 8], F32, name="wbc")
+
+        wbT = accp.tile([P, 512], F32, tag="acc", name="wbT")
+        nc.tensor.transpose(wbT[:, 0:P], wb_raw[:].bitcast(F32), ident[:])
+        nc.vector.tensor_copy(out=wbc[:], in_=wbT[:, 0:4].bitcast(BF16))
+
+        def wprep(t):
+            wg = wgp.tile([P, 512, 2], F32, name="wg", align_bytes=64)
+            for half in range(2):
+                wt = accp.tile([P, 2, 256], F32, tag="acc", name="wt")
+                for rr in range(2):
+                    words = w_sb[:, 4 * t + 2 * half + rr, :].bitcast(F32)
+                    for u in range(2):
+                        nc.tensor.transpose(
+                            wt[:, u, P * rr : P * rr + P], words[:, P * u : P * u + P], ident[:]
+                        )
+                nc.scalar.copy(
+                    out=wg[:, 256 * half : 256 * half + 256, :],
+                    in_=wt[:].rearrange("p u n -> p n u"),
+                )
+            nc.vector.quantize_mx(
+                out=wcodes[:, 512 * t : 512 * t + 512].bitcast(FP8X4),
+                scales=wscales[:, 512 * t : 512 * t + 512],
+                in_=wg[:].rearrange("p n u -> p (n u)").bitcast(BF16),
+            )
+
+        state = {}
+
+        def stats(g):
+            b, j0 = g // 2, G * (g % 2)
+            st = sp.tile([P, G, 6], F32, name="st")
+            mv = sp.tile([P, G, 2], F32, name="mv")
+            for i in range(G):
+                nc.vector.bn_stats(out=st[:, i, :], in_=x_sb[b][:, j0 + i, :])
+                nc.vector.bn_aggr(out=mv[:, i, :], in_=st[:, i, :])
+            ve = sp.tile([P, G, 1], F32, name="ve")
+            nc.vector.tensor_scalar_add(out=ve[:], in0=mv[:, :, 1:2], scalar1=EPS)
+            state[("mv", g)] = mv
+            state[("ve", g)] = ve
+
+        def rsq(g):
+            std = sp.tile([P, G, 1], F32, name="std")
+            nc.scalar.activation(out=std[:], in_=state[("ve", g)][:], func=ACT.Sqrt)
+            state[("std", g)] = std
+
+        def norm(g):
+            b, j0 = g // 2, G * (g % 2)
+            mv = state[("mv", g)]
+            rstd = sp.tile([P, G, 1], F32, name="rstd")
+            nc.vector.reciprocal(out=rstd[:], in_=state[("std", g)][:])
+            xns = []
+            for i in range(G):
+                xn = xnp.tile([P, E], F32, name="xn")
+                nc.vector.tensor_scalar(
+                    out=xn[:].rearrange("p (u e q) -> p u e q", u=2, e=2),
+                    in0=x_sb[b][:, j0 + i, :].rearrange("p (u q e) -> p u e q", u=2, e=2),
+                    scalar1=mv[:, i, 0:1],
+                    scalar2=rstd[:, i, 0:1],
+                    op0=ALU.subtract,
+                    op1=ALU.mult,
+                )
+                xns.append(xn)
+            state[("xn", g)] = xns
+
+        def flip(g):
+            xts = [xtp.tile([P, 512], F32, name="xt%d" % t) for t in range(4)]
+            for i in range(G):
+                xn = state[("xn", g)][i]
+                for t in range(4):
+                    nc.tensor.transpose(
+                        xts[t][:, P * i : P * i + P], xn[:, P * t : P * t + P], ident[:]
+                    )
+            state[("xt", g)] = xts
+
+        def affine(g, n_scalar):
+            pl = plp.tile([P, 4, 512], BF16, name="pl")
+            xts = state[("xt", g)]
+            for t in range(4):
+                if t < n_scalar:
+                    nc.scalar.activation(
+                        out=pl[:, t, :], in_=xts[t][:], func=ACT.Identity,
+                        bias=wbc[:, 4 + t : 5 + t], scale=wbc[:, t : t + 1],
+                    )
+                else:
+                    nc.vector.tensor_scalar(
+                        out=pl[:, t, :], in0=xts[t][:],
+                        scalar1=wbc[:, t : t + 1], scalar2=wbc[:, 4 + t : 5 + t],
+                        op0=ALU.mult, op1=ALU.add,
+                    )
+            state[("pl", g)] = pl
+
+        def regroup(g):
+            gr = grp.tile([P, 512, 4], BF16, name="gr", align_bytes=64)
+            nc.vector.tensor_copy(
+                out=gr[:].rearrange("p (c i) t -> p c t i", i=4),
+                in_=state[("pl", g)][:].rearrange("p t (c i) -> p c t i", i=4),
+            )
+            state[("gr", g)] = gr
+
+        def quant(g):
+            nc.vector.quantize_mx(
+                out=xc[g][:].bitcast(FP8X4),
+                scales=xs[g][:],
+                in_=state[("gr", g)][:].rearrange("p c t -> p (c t)"),
+            )
+
+        count = [0]
+
+        def passes(b, t3, js, ost, jbase, v_every):
+            for j in js:
+                g, i = 2 * b + j // G, j % G
+                acc = accp.tile([P, 512], F32, tag="acc", name="acc")
+                nc.tensor.matmul_mx(
+                    out=acc[:],
+                    lhsT=xc[g][:, P * i : P * i + P].bitcast(FP8X4),
+                    lhsT_scale=xs[g][:, P * i : P * i + P],
+                    rhs=wcodes[:, 512 * t3 : 512 * t3 + 512].bitcast(FP8X4),
+                    rhs_scale=wscales[:, 512 * t3 : 512 * t3 + 512],
+                    start=True,
+                    stop=True,
+                )
+                src = acc[:].rearrange("p (h d) -> p h d", h=H)
+                count[0] += 1
+                if count[0] % v_every == 0:
+                    nc.vector.tensor_copy(out=ost[:, :, j - jbase, :], in_=src)
+                else:
+                    nc.scalar.copy(out=ost[:, :, j - jbase, :], in_=src)
+
+        def store(b, t3, j0, nj, ost):
+            nc.sync.dma_start(
+                out=outs[t3][b].rearrange("h (p j) d -> p h j d", j=J)[:, :, j0 : j0 + nj, :],
+                in_=ost[:],
+            )
+
+        pieces = []
+
+        def half_unit(b, t3, j0, v_every):
+            ost = osp.tile([P, H, G, DH], F32, tag="ost", name="osth")
+            passes(b, t3, range(j0, j0 + G), ost, j0, v_every)
+            store(b, t3, j0, G, ost)
+
+        def full_first(b, t3, v_every):
+            ost = osp.tile([P, H, J, DH], F32, tag="ost", name="ost")
+            state[("ost", b, t3)] = ost
+            passes(b, t3, range(0, G), ost, 0, v_every)
+
+        def full_second(b, t3, v_every):
+            ost = state[("ost", b, t3)]
+            passes(b, t3, range(G, J), ost, 0, v_every)
+            store(b, t3, 0, J, ost)
+
+        for b in range(NB):
+            for t3 in range(3):
+                if b in (1, 2):
+                    pieces.append((2 * b + 3, full_first, (b, t3)))
+                    pieces.append((2 * b + 3, full_second, (b, t3)))
+            for g in range(2):
+                for t3 in range(3):
+                    if b in (0, 3):
+                        pieces.append((2 * b + g + 2, half_unit, (b, t3, G * g)))
+
+        stats(0)
+        rsq(0)
+        norm(0)
+        flip(0)
+        wprep(0)
+        step = 1
+        nxt = 0
+        while nxt < len(pieces) or step <= NG:
+            if step < NG:
+                stats(step)
+                rsq(step)
+            if step <= NG:
+                affine(step - 1, 4)
+                regroup(step - 1)
+            if step == 1:
+                wprep(1)
+                wprep(2)
+            done = 0
+            while nxt < len(pieces) and done < 3 and pieces[nxt][0] <= step:
+                fn, args = pieces[nxt][1], pieces[nxt][2]
+                fn(*args, 2 if step > NG else 5)
+                done += 1
+                nxt += 1
+            if step < NG:
+                norm(step)
+                flip(step)
+            if step <= NG:
+                quant(step - 1)
+            step += 1

@@ -16,170 +16,289 @@ ACT = mybir.ActivationFunctionType
 P = 128
 NB, SEQ, E, H, DH = 4, 1024, 512, 8, 64
 J = SEQ // P
-G = 4
-NG = NB * J // G
 EPS = 1e-5
+GROUPS = ((0, 0, 4), (0, 4, 4), (1, 0, 4), (1, 4, 4), (2, 0, 4), (2, 4, 4), (3, 0, 4), (3, 4, 4))
+XN_ENG = "VVVVVVVV"
+RG_ENG = "VVVVVVVV"
+PINNED = True
+ORDER = (
+    ("ident",), ("memset",), ("ldx", 0, 0, 4), ("ldwb",), ("ldw", 0), ("ldx", 0, 4, 4),
+    ("ldw", 1), ("ldw", 2), ("ldx", 1, 0, 8), ("ldx", 2, 0, 8), ("ldx", 3, 0, 8), ("bn", 0, 0),
+    ("wbT",), ("bn", 0, 1), ("bn", 0, 2), ("wt", 0, 0, 0), ("wt", 0, 0, 1), ("wt", 0, 0, 2),
+    ("bn", 0, 3), ("wt", 0, 0, 3), ("wt", 0, 1, 0), ("wt", 0, 1, 1), ("we", 0, 0, "S"), ("wt", 0, 1, 2),
+    ("wt", 0, 1, 3), ("ag", 0, 0), ("ag", 0, 1), ("ag", 0, 2), ("we", 0, 1, "S"), ("ag", 0, 3),
+    ("ve", 0), ("wbc",), ("bn", 1, 0), ("sq", 0), ("rc", 0), ("xn", 0, 0),
+    ("xn", 0, 1), ("tr", 0, 0, 0), ("tr", 0, 0, 1), ("tr", 0, 0, 2), ("xn", 0, 2), ("tr", 0, 0, 3),
+    ("tr", 0, 1, 0), ("tr", 0, 1, 1), ("xn", 0, 3), ("tr", 0, 1, 2), ("tr", 0, 1, 3), ("tr", 0, 2, 0),
+    ("tr", 0, 2, 1), ("wq", 0), ("tr", 0, 2, 2), ("tr", 0, 2, 3), ("tr", 0, 3, 0), ("tr", 0, 3, 1),
+    ("tr", 0, 3, 2), ("C", 0, 0, "S"), ("tr", 0, 3, 3), ("wt", 1, 0, 0), ("bn", 1, 1), ("wt", 1, 0, 1),
+    ("wt", 1, 0, 2), ("wt", 1, 0, 3), ("wt", 1, 1, 0), ("wt", 1, 1, 1), ("C", 0, 1, "S"), ("wt", 1, 1, 2),
+    ("wt", 1, 1, 3), ("bn", 1, 2), ("wt", 2, 0, 0), ("wt", 2, 0, 1), ("wt", 2, 0, 2), ("wt", 2, 0, 3),
+    ("wt", 2, 1, 0), ("C", 0, 2, "S"), ("wt", 2, 1, 1), ("wt", 2, 1, 2), ("bn", 1, 3), ("wt", 2, 1, 3),
+    ("C", 0, 3, "S"), ("ag", 1, 0), ("ag", 1, 1), ("ag", 1, 2), ("ag", 1, 3), ("ve", 1),
+    ("we", 1, 0, "V"), ("we", 1, 1, "S"), ("rg", 0), ("we", 2, 0, "S"), ("we", 2, 1, "S"), ("q", 0),
+    ("sq", 1), ("wq", 1), ("mx", 0, 0, 0), ("rc", 1), ("xn", 1, 0), ("mx", 0, 0, 1),
+    ("ev", 0, 0, 0, 0, 4, "S"), ("xn", 1, 1), ("mx", 0, 0, 2), ("xn", 1, 2), ("mx", 0, 0, 3), ("ev", 0, 0, 1, 0, 4, "S"),
+    ("xn", 1, 3), ("mx", 0, 1, 0), ("tr", 1, 0, 0), ("wq", 2), ("ev", 0, 0, 2, 0, 4, "S"), ("mx", 0, 1, 1),
+    ("ev", 0, 0, 3, 0, 4, "V"), ("tr", 1, 0, 1), ("ev", 0, 1, 0, 0, 4, "S"), ("mx", 0, 1, 2), ("bn", 2, 0), ("ev", 0, 1, 1, 0, 4, "S"),
+    ("st", 0, 0, 0, 4), ("mx", 0, 1, 3), ("tr", 1, 0, 2), ("bn", 2, 1), ("tr", 1, 0, 3), ("ev", 0, 1, 2, 0, 4, "S"),
+    ("tr", 1, 1, 0), ("tr", 1, 1, 1), ("tr", 1, 1, 2), ("tr", 1, 1, 3), ("tr", 1, 2, 0), ("tr", 1, 2, 1),
+    ("bn", 2, 2), ("tr", 1, 2, 2), ("ev", 0, 1, 3, 0, 4, "S"), ("tr", 1, 2, 3), ("tr", 1, 3, 0), ("tr", 1, 3, 1),
+    ("tr", 1, 3, 2), ("tr", 1, 3, 3), ("mx", 0, 2, 0), ("bn", 2, 3), ("C", 1, 0, "S"), ("st", 0, 1, 0, 4),
+    ("mx", 0, 2, 1), ("ag", 2, 0), ("C", 1, 1, "S"), ("ag", 2, 1), ("mx", 0, 2, 2), ("ag", 2, 2),
+    ("ag", 2, 3), ("ve", 2), ("mx", 0, 2, 3), ("bn", 3, 0), ("C", 1, 2, "S"), ("bn", 3, 1),
+    ("C", 1, 3, "S"), ("bn", 3, 2), ("ev", 0, 2, 0, 0, 4, "S"), ("rg", 1), ("ev", 0, 2, 1, 0, 4, "S"), ("ev", 0, 2, 2, 0, 4, "S"),
+    ("q", 1), ("ev", 0, 2, 3, 0, 4, "S"), ("bn", 3, 3), ("sq", 2), ("st", 0, 2, 0, 4), ("mx", 0, 0, 4),
+    ("rc", 2), ("mx", 0, 0, 5), ("xn", 2, 0), ("ev", 0, 0, 4, 4, 4, "S"), ("mx", 0, 0, 6), ("xn", 2, 1),
+    ("mx", 0, 0, 7), ("xn", 2, 2), ("ev", 0, 0, 5, 4, 4, "S"), ("mx", 0, 1, 4), ("xn", 2, 3), ("tr", 2, 0, 0),
+    ("ev", 0, 0, 6, 4, 4, "S"), ("ag", 3, 0), ("ag", 3, 1), ("mx", 0, 1, 5), ("ag", 3, 2), ("ag", 3, 3),
+    ("ve", 3), ("ev", 0, 0, 7, 4, 4, "V"), ("tr", 2, 0, 1), ("ev", 0, 1, 4, 4, 4, "S"), ("mx", 0, 1, 6), ("ev", 0, 1, 5, 4, 4, "V"),
+    ("st", 0, 0, 4, 4), ("sq", 3), ("mx", 0, 1, 7), ("ev", 0, 1, 6, 4, 4, "S"), ("tr", 2, 0, 2), ("rc", 3),
+    ("tr", 2, 0, 3), ("xn", 3, 0), ("tr", 2, 1, 0), ("tr", 2, 1, 1), ("ev", 0, 1, 7, 4, 4, "S"), ("tr", 2, 1, 2),
+    ("tr", 2, 1, 3), ("xn", 3, 1), ("tr", 2, 2, 0), ("tr", 2, 2, 1), ("tr", 2, 2, 2), ("xn", 3, 2),
+    ("tr", 2, 2, 3), ("tr", 2, 3, 0), ("tr", 2, 3, 1), ("st", 0, 1, 4, 4), ("tr", 2, 3, 2), ("C", 2, 0, "S"),
+    ("xn", 3, 3), ("tr", 2, 3, 3), ("mx", 0, 2, 4), ("C", 2, 1, "V"), ("mx", 0, 2, 5), ("C", 2, 2, "S"),
+    ("tr", 3, 0, 0), ("C", 2, 3, "V"), ("tr", 3, 0, 1), ("tr", 3, 1, 0), ("ev", 0, 2, 4, 4, 4, "S"), ("tr", 3, 1, 1),
+    ("tr", 3, 0, 2), ("tr", 3, 1, 2), ("tr", 3, 2, 0), ("rg", 2), ("tr", 3, 0, 3), ("tr", 3, 1, 3),
+    ("tr", 3, 2, 1), ("ev", 0, 2, 5, 4, 4, "S"), ("tr", 3, 2, 2), ("tr", 3, 2, 3), ("tr", 3, 3, 0), ("tr", 3, 3, 1),
+    ("tr", 3, 3, 2), ("tr", 3, 3, 3), ("mx", 0, 2, 6), ("C", 3, 0, "S"), ("q", 2), ("mx", 0, 2, 7),
+    ("C", 3, 1, "S"), ("C", 3, 2, "V"), ("C", 3, 3, "S"), ("mx", 1, 0, 0), ("ev", 0, 2, 6, 4, 4, "V"), ("mx", 1, 0, 1),
+    ("ev", 0, 2, 7, 4, 4, "S"), ("rg", 3), ("mx", 1, 0, 2), ("ev", 1, 0, 0, 0, 8, "S"), ("st", 0, 2, 4, 4), ("mx", 1, 0, 3),
+    ("ev", 1, 0, 1, 0, 8, "S"), ("q", 3), ("ev", 1, 0, 2, 0, 8, "S"), ("ev", 1, 0, 3, 0, 8, "V"), ("mx", 1, 0, 4), ("bn", 4, 0),
+    ("mx", 1, 0, 5), ("ev", 1, 0, 4, 0, 8, "S"), ("mx", 1, 0, 6), ("ev", 1, 0, 5, 0, 8, "V"), ("mx", 1, 0, 7), ("ev", 1, 0, 6, 0, 8, "S"),
+    ("mx", 1, 1, 0), ("ev", 1, 0, 7, 0, 8, "V"), ("mx", 1, 1, 1), ("ev", 1, 1, 0, 0, 8, "S"), ("mx", 1, 1, 2), ("bn", 4, 1),
+    ("st", 1, 0, 0, 8), ("mx", 1, 1, 3), ("ev", 1, 1, 1, 0, 8, "S"), ("mx", 1, 1, 4), ("bn", 4, 2), ("ev", 1, 1, 2, 0, 8, "S"),
+    ("mx", 1, 1, 5), ("bn", 4, 3), ("ev", 1, 1, 3, 0, 8, "S"), ("mx", 1, 1, 6), ("ag", 4, 0), ("ag", 4, 1),
+    ("ev", 1, 1, 4, 0, 8, "S"), ("ag", 4, 2), ("ag", 4, 3), ("mx", 1, 1, 7), ("ve", 4), ("bn", 5, 0),
+    ("ev", 1, 1, 5, 0, 8, "S"), ("mx", 1, 2, 0), ("bn", 5, 1), ("ev", 1, 1, 6, 0, 8, "S"), ("mx", 1, 2, 1), ("bn", 5, 2),
+    ("ev", 1, 1, 7, 0, 8, "S"), ("mx", 1, 2, 2), ("bn", 5, 3), ("ev", 1, 2, 0, 0, 8, "S"), ("st", 1, 1, 0, 8), ("mx", 1, 2, 3),
+    ("ag", 5, 0), ("ag", 5, 1), ("ag", 5, 2), ("ag", 5, 3), ("ev", 1, 2, 1, 0, 8, "S"), ("ve", 5),
+    ("mx", 1, 2, 4), ("ev", 1, 2, 2, 0, 8, "V"), ("ev", 1, 2, 3, 0, 8, "S"), ("mx", 1, 2, 5), ("ev", 1, 2, 4, 0, 8, "V"), ("mx", 1, 2, 6),
+    ("sq", 4), ("ev", 1, 2, 5, 0, 8, "S"), ("mx", 1, 2, 7), ("rc", 4), ("xn", 4, 0), ("xn", 4, 1),
+    ("ev", 1, 2, 6, 0, 8, "S"), ("tr", 4, 0, 0), ("xn", 4, 2), ("tr", 4, 0, 1), ("tr", 4, 0, 2), ("tr", 4, 0, 3),
+    ("tr", 4, 1, 0), ("xn", 4, 3), ("ev", 1, 2, 7, 0, 8, "S"), ("tr", 4, 1, 1), ("tr", 4, 1, 2), ("tr", 4, 1, 3),
+    ("tr", 4, 2, 0), ("bn", 6, 0), ("tr", 4, 2, 1), ("tr", 4, 2, 2), ("tr", 4, 2, 3), ("sq", 5),
+    ("tr", 4, 3, 0), ("st", 1, 2, 0, 8), ("tr", 4, 3, 1), ("tr", 4, 3, 2), ("C", 4, 0, "S"), ("rc", 5),
+    ("tr", 4, 3, 3), ("xn", 5, 0), ("xn", 5, 1), ("C", 4, 1, "S"), ("tr", 5, 0, 0), ("xn", 5, 2),
+    ("tr", 5, 1, 0), ("xn", 5, 3), ("tr", 5, 2, 0), ("C", 4, 2, "S"), ("tr", 5, 0, 1), ("C", 4, 3, "V"),
+    ("tr", 5, 1, 1), ("tr", 5, 2, 1), ("tr", 5, 3, 0), ("tr", 5, 3, 1), ("C", 5, 0, "S"), ("tr", 5, 0, 2),
+    ("rg", 4), ("tr", 5, 0, 3), ("tr", 5, 1, 2), ("tr", 5, 1, 3), ("tr", 5, 2, 2), ("tr", 5, 2, 3),
+    ("C", 5, 1, "S"), ("tr", 5, 3, 2), ("tr", 5, 3, 3), ("C", 5, 2, "S"), ("q", 4), ("C", 5, 3, "S"),
+    ("bn", 6, 1), ("mx", 2, 0, 0), ("rg", 5), ("mx", 2, 0, 1), ("ev", 2, 0, 0, 0, 8, "S"), ("mx", 2, 0, 2),
+    ("mx", 2, 0, 3), ("ev", 2, 0, 1, 0, 8, "S"), ("q", 5), ("ev", 2, 0, 2, 0, 8, "S"), ("ev", 2, 0, 3, 0, 8, "V"), ("mx", 2, 0, 4),
+    ("bn", 6, 2), ("mx", 2, 0, 5), ("ev", 2, 0, 4, 0, 8, "S"), ("mx", 2, 0, 6), ("ev", 2, 0, 5, 0, 8, "V"), ("mx", 2, 0, 7),
+    ("ev", 2, 0, 6, 0, 8, "S"), ("mx", 2, 1, 0), ("ev", 2, 0, 7, 0, 8, "V"), ("mx", 2, 1, 1), ("ev", 2, 1, 0, 0, 8, "S"), ("mx", 2, 1, 2),
+    ("bn", 6, 3), ("st", 2, 0, 0, 8), ("mx", 2, 1, 3), ("ev", 2, 1, 1, 0, 8, "S"), ("mx", 2, 1, 4), ("ag", 6, 0),
+    ("ag", 6, 1), ("ag", 6, 2), ("ev", 2, 1, 2, 0, 8, "S"), ("ag", 6, 3), ("mx", 2, 1, 5), ("ve", 6),
+    ("bn", 7, 0), ("ev", 2, 1, 3, 0, 8, "S"), ("mx", 2, 1, 6), ("bn", 7, 1), ("ev", 2, 1, 4, 0, 8, "S"), ("mx", 2, 1, 7),
+    ("bn", 7, 2), ("ev", 2, 1, 5, 0, 8, "S"), ("mx", 2, 2, 0), ("bn", 7, 3), ("ev", 2, 1, 6, 0, 8, "S"), ("mx", 2, 2, 1),
+    ("ag", 7, 0), ("ag", 7, 1), ("ag", 7, 2), ("ag", 7, 3), ("ev", 2, 1, 7, 0, 8, "S"), ("ve", 7),
+    ("mx", 2, 2, 2), ("ev", 2, 2, 0, 0, 8, "V"), ("ev", 2, 2, 1, 0, 8, "S"), ("st", 2, 1, 0, 8), ("mx", 2, 2, 3), ("ev", 2, 2, 2, 0, 8, "V"),
+    ("mx", 2, 2, 4), ("ev", 2, 2, 3, 0, 8, "S"), ("mx", 2, 2, 5), ("ev", 2, 2, 4, 0, 8, "V"), ("mx", 2, 2, 6), ("sq", 6),
+    ("ev", 2, 2, 5, 0, 8, "S"), ("mx", 2, 2, 7), ("rc", 6), ("xn", 6, 0), ("xn", 6, 1), ("ev", 2, 2, 6, 0, 8, "S"),
+    ("tr", 6, 0, 0), ("xn", 6, 2), ("tr", 6, 0, 1), ("tr", 6, 0, 2), ("tr", 6, 0, 3), ("tr", 6, 1, 0),
+    ("ev", 2, 2, 7, 0, 8, "S"), ("xn", 6, 3), ("tr", 6, 1, 1), ("tr", 6, 1, 2), ("tr", 6, 1, 3), ("tr", 6, 2, 0),
+    ("tr", 6, 2, 1), ("tr", 6, 2, 2), ("tr", 6, 2, 3), ("sq", 7), ("tr", 6, 3, 0), ("st", 2, 2, 0, 8),
+    ("tr", 6, 3, 1), ("rc", 7), ("tr", 6, 3, 2), ("C", 6, 0, "S"), ("xn", 7, 0), ("tr", 6, 3, 3),
+    ("xn", 7, 1), ("C", 6, 1, "S"), ("xn", 7, 2), ("tr", 7, 0, 0), ("tr", 7, 1, 0), ("xn", 7, 3),
+    ("tr", 7, 2, 0), ("C", 6, 2, "S"), ("C", 6, 3, "V"), ("tr", 7, 0, 1), ("tr", 7, 1, 1), ("tr", 7, 2, 1),
+    ("tr", 7, 3, 0), ("tr", 7, 3, 1), ("C", 7, 0, "V"), ("C", 7, 1, "S"), ("tr", 7, 0, 2), ("tr", 7, 0, 3),
+    ("tr", 7, 1, 2), ("tr", 7, 1, 3), ("tr", 7, 2, 2), ("tr", 7, 2, 3), ("rg", 6), ("tr", 7, 3, 2),
+    ("tr", 7, 3, 3), ("C", 7, 2, "S"), ("C", 7, 3, "S"), ("q", 6), ("rg", 7), ("mx", 3, 0, 0),
+    ("mx", 3, 0, 1), ("ev", 3, 0, 0, 0, 8, "S"), ("mx", 3, 0, 2), ("q", 7), ("mx", 3, 0, 3), ("ev", 3, 0, 1, 0, 8, "S"),
+    ("ev", 3, 0, 2, 0, 8, "V"), ("ev", 3, 0, 3, 0, 8, "S"), ("mx", 3, 0, 4), ("mx", 3, 0, 5), ("ev", 3, 0, 4, 0, 8, "V"), ("mx", 3, 0, 6),
+    ("ev", 3, 0, 5, 0, 8, "S"), ("mx", 3, 0, 7), ("ev", 3, 0, 6, 0, 8, "V"), ("mx", 3, 1, 0), ("ev", 3, 0, 7, 0, 8, "S"), ("mx", 3, 1, 1),
+    ("ev", 3, 1, 0, 0, 8, "V"), ("mx", 3, 1, 2), ("ev", 3, 1, 1, 0, 8, "S"), ("st", 3, 0, 0, 8), ("mx", 3, 1, 3), ("ev", 3, 1, 2, 0, 8, "V"),
+    ("mx", 3, 1, 4), ("ev", 3, 1, 3, 0, 8, "S"), ("mx", 3, 1, 5), ("ev", 3, 1, 4, 0, 8, "V"), ("mx", 3, 1, 6), ("ev", 3, 1, 5, 0, 8, "S"),
+    ("mx", 3, 1, 7), ("ev", 3, 1, 6, 0, 8, "V"), ("mx", 3, 2, 0), ("ev", 3, 1, 7, 0, 8, "S"), ("mx", 3, 2, 1), ("ev", 3, 2, 0, 0, 8, "V"),
+    ("mx", 3, 2, 2), ("ev", 3, 2, 1, 0, 8, "S"), ("st", 3, 1, 0, 8), ("mx", 3, 2, 3), ("ev", 3, 2, 2, 0, 8, "V"), ("mx", 3, 2, 4),
+    ("ev", 3, 2, 3, 0, 8, "S"), ("mx", 3, 2, 5), ("ev", 3, 2, 4, 0, 8, "V"), ("mx", 3, 2, 6), ("ev", 3, 2, 5, 0, 8, "S"), ("mx", 3, 2, 7),
+    ("ev", 3, 2, 6, 0, 8, "V"), ("ev", 3, 2, 7, 0, 8, "S"), ("st", 3, 2, 0, 8),
+)
 
 
 def tile_selfattention_pa_t_kernel(tc, inputs, ln_w, ln_b, w_qkv, out_0, out_1, out_2):
     nc = tc.nc
     outs = (out_0, out_1, out_2)
+    ng = len(GROUPS)
     with ExitStack() as ctx:
         keep = ctx.enter_context(tc.tile_pool(name="keep", bufs=1))
         wgp = ctx.enter_context(tc.tile_pool(name="wgp", bufs=2))
-        sp = ctx.enter_context(tc.tile_pool(name="sp", bufs=4))
+        sp = ctx.enter_context(tc.tile_pool(name="sp", bufs=8))
         xnp = ctx.enter_context(tc.tile_pool(name="xnp", bufs=8))
         plp = ctx.enter_context(tc.tile_pool(name="plp", bufs=2))
         grp = ctx.enter_context(tc.tile_pool(name="grp", bufs=2))
-        osp = ctx.enter_context(tc.tile_pool(name="osp", bufs=6))
+        osp = ctx.enter_context(tc.tile_pool(name="osp", bufs=7))
         xtp = ctx.enter_context(tc.psum_pool(name="xtp", bufs=1))
         accp = ctx.enter_context(tc.psum_pool(name="accp", bufs=4))
+        if PINNED:
+            ctx.enter_context(tc.manual_schedule())
 
         wb_raw = keep.tile([P, 2 * P], BF16, name="wb_raw")
-        nc.vector.memset(wb_raw[:], 0.0)
         one_t = keep.tile([P, 1], F32, name="one_t")
-        nc.vector.memset(one_t[:], 1.0)
         junk = keep.tile([P, 1], F32, name="junk")
-        nc.scalar.activation(out=junk[:], in_=one_t[:], func=ACT.Sqrt)
         ident = keep.tile([P, P], F32, name="ident")
-        make_identity(nc, ident[:])
-
         x_sb = [keep.tile([P, J, E], BF16, name="x%d" % b) for b in range(NB)]
         w_sb = keep.tile([P, 12, E], BF16, name="w_sb")
         xv = [inputs[b].rearrange("(p j) k -> p j k", j=J) for b in range(NB)]
-
-        def load_w(t):
-            nc.sync.dma_start(
-                out=w_sb[:, 4 * t : 4 * t + 4, :],
-                in_=w_qkv[512 * t : 512 * t + 512, :].rearrange("(r p) k -> p r k", p=P),
-            )
-
-        nc.sync.dma_start(out=x_sb[0][:, 0:4, :], in_=xv[0][:, 0:4, :])
-        nc.sync.dma_start(out=wb_raw[0:2, :], in_=ln_w.rearrange("(u c) -> u c", u=2))
-        nc.sync.dma_start(out=wb_raw[2:4, :], in_=ln_b.rearrange("(u c) -> u c", u=2))
-        load_w(0)
-        nc.sync.dma_start(out=x_sb[0][:, 4:8, :], in_=xv[0][:, 4:8, :])
-        load_w(1)
-        load_w(2)
-        for b in range(1, NB):
-            nc.sync.dma_start(out=x_sb[b][:], in_=xv[b])
-
         wcodes = keep.tile([P, 1536], U32, name="wcodes", align_bytes=64)
         wscales = keep.tile([P, 1536], U8, name="wscales", align_bytes=64)
-        xc = [keep.tile([P, 512], U32, name="xc%d" % g, align_bytes=64) for g in range(NG)]
-        xs = [keep.tile([P, 512], U8, name="xs%d" % g, align_bytes=64) for g in range(NG)]
+        xc = [keep.tile([P, P * GROUPS[g][2]], U32, name="xc%d" % g, align_bytes=64) for g in range(ng)]
+        xs = [keep.tile([P, P * GROUPS[g][2]], U8, name="xs%d" % g, align_bytes=64) for g in range(ng)]
         wbc = keep.tile([P, 8], F32, name="wbc")
+        st = {}
 
-        wbT = accp.tile([P, 512], F32, tag="acc", name="wbT")
-        nc.tensor.transpose(wbT[:, 0:P], wb_raw[:].bitcast(F32), ident[:])
-        nc.vector.tensor_copy(out=wbc[:], in_=wbT[:, 0:4].bitcast(BF16))
+        def group_of(b, j):
+            for g in range(ng):
+                if GROUPS[g][0] == b and GROUPS[g][1] <= j < GROUPS[g][1] + GROUPS[g][2]:
+                    return g
+            return -1
 
-        def wprep(t):
-            wg = wgp.tile([P, 512, 2], F32, name="wg", align_bytes=64)
-            for half in range(2):
-                wt = accp.tile([P, 2, 256], F32, tag="acc", name="wt")
-                for rr in range(2):
-                    words = w_sb[:, 4 * t + 2 * half + rr, :].bitcast(F32)
-                    for u in range(2):
-                        nc.tensor.transpose(
-                            wt[:, u, P * rr : P * rr + P], words[:, P * u : P * u + P], ident[:]
-                        )
-                nc.scalar.copy(
-                    out=wg[:, 256 * half : 256 * half + 256, :],
-                    in_=wt[:].rearrange("p u n -> p n u"),
+        def get(key, make):
+            if key not in st:
+                st[key] = make()
+            return st[key]
+
+        def emit(tok):
+            k = tok[0]
+            a = [v for v in tok[1:] if v not in ("S", "V")]
+            eng = tok[-1]
+            if k == "ident":
+                make_identity(nc, ident[:])
+            elif k == "memset":
+                nc.vector.memset(wb_raw[:], 0.0)
+                nc.vector.memset(one_t[:], 1.0)
+                nc.scalar.activation(out=junk[:], in_=one_t[:], func=ACT.Sqrt)
+            elif k == "ldwb":
+                nc.sync.dma_start(out=wb_raw[0:2, :], in_=ln_w.rearrange("(u c) -> u c", u=2))
+                nc.sync.dma_start(out=wb_raw[2:4, :], in_=ln_b.rearrange("(u c) -> u c", u=2))
+            elif k == "ldw":
+                t = a[0]
+                nc.sync.dma_start(
+                    out=w_sb[:, 4 * t : 4 * t + 4, :],
+                    in_=w_qkv[512 * t : 512 * t + 512, :].rearrange("(r p) k -> p r k", p=P),
                 )
-            nc.vector.quantize_mx(
-                out=wcodes[:, 512 * t : 512 * t + 512].bitcast(FP8X4),
-                scales=wscales[:, 512 * t : 512 * t + 512],
-                in_=wg[:].rearrange("p n u -> p (n u)").bitcast(BF16),
-            )
-
-        state = {}
-
-        def stats(g):
-            b, j0 = g // 2, G * (g % 2)
-            st = sp.tile([P, G, 6], F32, name="st")
-            mv = sp.tile([P, G, 2], F32, name="mv")
-            for i in range(G):
-                nc.vector.bn_stats(out=st[:, i, :], in_=x_sb[b][:, j0 + i, :])
-                nc.vector.bn_aggr(out=mv[:, i, :], in_=st[:, i, :])
-            ve = sp.tile([P, G, 1], F32, name="ve")
-            nc.vector.tensor_scalar_add(out=ve[:], in0=mv[:, :, 1:2], scalar1=EPS)
-            state[("mv", g)] = mv
-            state[("ve", g)] = ve
-
-        def rsq(g):
-            std = sp.tile([P, G, 1], F32, name="std")
-            nc.scalar.activation(out=std[:], in_=state[("ve", g)][:], func=ACT.Sqrt)
-            state[("std", g)] = std
-
-        def norm(g):
-            b, j0 = g // 2, G * (g % 2)
-            mv = state[("mv", g)]
-            rstd = sp.tile([P, G, 1], F32, name="rstd")
-            nc.vector.reciprocal(out=rstd[:], in_=state[("std", g)][:])
-            xns = []
-            for i in range(G):
+            elif k == "ldx":
+                b, j0, n = a
+                nc.sync.dma_start(out=x_sb[b][:, j0 : j0 + n, :], in_=xv[b][:, j0 : j0 + n, :])
+            elif k == "wbT":
+                wbT = accp.tile([P, 512], F32, tag="acc", name="wbT")
+                st["wbT"] = wbT
+                nc.tensor.transpose(wbT[:, 0:P], wb_raw[:].bitcast(F32), ident[:])
+            elif k == "wbc":
+                nc.vector.tensor_copy(out=wbc[:], in_=st["wbT"][:, 0:4].bitcast(BF16))
+            elif k == "wt":
+                t, half, i = a
+                wt = get(("wt", t, half), lambda: accp.tile([P, 2, 256], F32, tag="acc", name="wt"))
+                rr, u = i // 2, i % 2
+                words = w_sb[:, 4 * t + 2 * half + rr, :].bitcast(F32)
+                nc.tensor.transpose(wt[:, u, P * rr : P * rr + P], words[:, P * u : P * u + P], ident[:])
+            elif k == "we":
+                t, half = a
+                wg = get(("wg", t), lambda: wgp.tile([P, 512, 2], F32, name="wg", align_bytes=64))
+                dst = wg[:, 256 * half : 256 * half + 256, :]
+                src = st[("wt", t, half)][:].rearrange("p u n -> p n u")
+                if eng == "S":
+                    nc.scalar.copy(out=dst, in_=src)
+                else:
+                    nc.vector.tensor_copy(out=dst, in_=src)
+            elif k == "wq":
+                t = a[0]
+                nc.vector.quantize_mx(
+                    out=wcodes[:, 512 * t : 512 * t + 512].bitcast(FP8X4),
+                    scales=wscales[:, 512 * t : 512 * t + 512],
+                    in_=st[("wg", t)][:].rearrange("p n u -> p (n u)").bitcast(BF16),
+                )
+            elif k == "bn":
+                g, i = a
+                b, j0, n = GROUPS[g]
+                sts = get(("st", g), lambda: sp.tile([P, 4, 6], F32, name="sts"))
+                nc.vector.bn_stats(out=sts[:, i, :], in_=x_sb[b][:, j0 + i, :])
+            elif k == "ag":
+                g, i = a
+                mv = get(("mv", g), lambda: sp.tile([P, 4, 2], F32, name="mv"))
+                nc.vector.bn_aggr(out=mv[:, i, :], in_=st[("st", g)][:, i, :])
+            elif k == "ve":
+                g = a[0]
+                n = GROUPS[g][2]
+                ve = sp.tile([P, 4, 1], F32, name="ve")
+                st[("ve", g)] = ve
+                nc.vector.tensor_scalar_add(out=ve[:, 0:n, :], in0=st[("mv", g)][:, 0:n, 1:2], scalar1=EPS)
+            elif k == "sq":
+                g = a[0]
+                n = GROUPS[g][2]
+                std = sp.tile([P, 4, 1], F32, name="std")
+                st[("std", g)] = std
+                nc.scalar.activation(out=std[:, 0:n, :], in_=st[("ve", g)][:, 0:n, :], func=ACT.Sqrt)
+            elif k == "rc":
+                g = a[0]
+                n = GROUPS[g][2]
+                rstd = sp.tile([P, 4, 1], F32, name="rstd")
+                st[("rstd", g)] = rstd
+                nc.vector.reciprocal(out=rstd[:, 0:n, :], in_=st[("std", g)][:, 0:n, :])
+                if XN_ENG[g] == "G":
+                    nmu = sp.tile([P, 4, 1], F32, name="nmu")
+                    st[("nmu", g)] = nmu
+                    nc.vector.tensor_scalar_mul(out=nmu[:, 0:n, :], in0=st[("mv", g)][:, 0:n, 0:1], scalar1=-1.0)
+            elif k == "xn":
+                g, i = a
+                b, j0, n = GROUPS[g]
                 xn = xnp.tile([P, E], F32, name="xn")
-                nc.vector.tensor_scalar(
-                    out=xn[:].rearrange("p (u e q) -> p u e q", u=2, e=2),
-                    in0=x_sb[b][:, j0 + i, :].rearrange("p (u q e) -> p u e q", u=2, e=2),
-                    scalar1=mv[:, i, 0:1],
-                    scalar2=rstd[:, i, 0:1],
-                    op0=ALU.subtract,
-                    op1=ALU.mult,
-                )
-                xns.append(xn)
-            state[("xn", g)] = xns
-
-        def flip(g):
-            xts = [xtp.tile([P, 512], F32, name="xt%d" % t) for t in range(4)]
-            for i in range(G):
-                xn = state[("xn", g)][i]
-                for t in range(4):
-                    nc.tensor.transpose(
-                        xts[t][:, P * i : P * i + P], xn[:, P * t : P * t + P], ident[:]
+                st[("xn", g, i)] = xn
+                dst = xn[:].rearrange("p (u e q) -> p u e q", u=2, e=2)
+                src = x_sb[b][:, j0 + i, :].rearrange("p (u q e) -> p u e q", u=2, e=2)
+                if XN_ENG[g] == "G":
+                    nc.gpsimd.tensor_scalar(
+                        out=dst, in0=src, scalar1=st[("nmu", g)][:, i, 0:1], scalar2=st[("rstd", g)][:, i, 0:1],
+                        op0=ALU.add, op1=ALU.mult,
                     )
-            state[("xt", g)] = xts
-
-        def affine(g, n_scalar):
-            pl = plp.tile([P, 4, 512], BF16, name="pl")
-            xts = state[("xt", g)]
-            for t in range(4):
-                if t < n_scalar:
+                else:
+                    nc.vector.tensor_scalar(
+                        out=dst, in0=src, scalar1=st[("mv", g)][:, i, 0:1], scalar2=st[("rstd", g)][:, i, 0:1],
+                        op0=ALU.subtract, op1=ALU.mult,
+                    )
+            elif k == "tr":
+                g, i, t = a
+                xt = get(("xt", g, t), lambda: xtp.tile([P, 512], F32, name="xt%d" % t))
+                nc.tensor.transpose(xt[:, P * i : P * i + P], st[("xn", g, i)][:, P * t : P * t + P], ident[:])
+            elif k == "C":
+                g, t = a
+                w = P * GROUPS[g][2]
+                pl = get(("pl", g), lambda: plp.tile([P, 4, 512], BF16, name="pl"))
+                if eng == "S":
                     nc.scalar.activation(
-                        out=pl[:, t, :], in_=xts[t][:], func=ACT.Identity,
+                        out=pl[:, t, 0:w], in_=st[("xt", g, t)][:, 0:w], func=ACT.Identity,
                         bias=wbc[:, 4 + t : 5 + t], scale=wbc[:, t : t + 1],
                     )
                 else:
                     nc.vector.tensor_scalar(
-                        out=pl[:, t, :], in0=xts[t][:],
-                        scalar1=wbc[:, t : t + 1], scalar2=wbc[:, 4 + t : 5 + t],
-                        op0=ALU.mult, op1=ALU.add,
+                        out=pl[:, t, 0:w], in0=st[("xt", g, t)][:, 0:w],
+                        scalar1=wbc[:, t : t + 1], scalar2=wbc[:, 4 + t : 5 + t], op0=ALU.mult, op1=ALU.add,
                     )
-            state[("pl", g)] = pl
-
-        def regroup(g):
-            gr = grp.tile([P, 512, 4], BF16, name="gr", align_bytes=64)
-            nc.vector.tensor_copy(
-                out=gr[:].rearrange("p (c i) t -> p c t i", i=4),
-                in_=state[("pl", g)][:].rearrange("p t (c i) -> p c t i", i=4),
-            )
-            state[("gr", g)] = gr
-
-        def quant(g):
-            nc.vector.quantize_mx(
-                out=xc[g][:].bitcast(FP8X4),
-                scales=xs[g][:],
-                in_=state[("gr", g)][:].rearrange("p c t -> p (c t)"),
-            )
-
-        count = [0]
-
-        def passes(b, t3, js, ost, jbase, v_every):
-            for j in js:
-                g, i = 2 * b + j // G, j % G
+            elif k == "rg":
+                g = a[0]
+                w = P * GROUPS[g][2]
+                gr = grp.tile([P, 512, 4], BF16, name="gr", align_bytes=64)
+                st[("gr", g)] = gr
+                dst = gr[:, 0:w, :].rearrange("p (c i) t -> p c t i", i=4)
+                src = st[("pl", g)][:, :, 0:w].rearrange("p t (c i) -> p c t i", i=4)
+                if RG_ENG[g] == "G":
+                    nc.gpsimd.tensor_scalar(out=dst, in0=src, scalar1=1.0, scalar2=0.0, op0=ALU.mult, op1=ALU.add)
+                else:
+                    nc.vector.tensor_copy(out=dst, in_=src)
+            elif k == "q":
+                g = a[0]
+                w = P * GROUPS[g][2]
+                nc.vector.quantize_mx(
+                    out=xc[g][:].bitcast(FP8X4), scales=xs[g][:],
+                    in_=st[("gr", g)][:, 0:w, :].rearrange("p c t -> p (c t)"),
+                )
+            elif k == "mx":
+                b, t3, j = a
+                g = group_of(b, j)
+                i = j - GROUPS[g][1]
                 acc = accp.tile([P, 512], F32, tag="acc", name="acc")
+                st[("acc", b, t3, j)] = acc
                 nc.tensor.matmul_mx(
                     out=acc[:],
                     lhsT=xc[g][:, P * i : P * i + P].bitcast(FP8X4),
@@ -189,72 +308,22 @@ def tile_selfattention_pa_t_kernel(tc, inputs, ln_w, ln_b, w_qkv, out_0, out_1, 
                     start=True,
                     stop=True,
                 )
-                src = acc[:].rearrange("p (h d) -> p h d", h=H)
-                count[0] += 1
-                if count[0] % v_every == 0:
-                    nc.vector.tensor_copy(out=ost[:, :, j - jbase, :], in_=src)
+            elif k == "ev":
+                b, t3, j, j0, n = a
+                ost = get(("ost", b, t3, j0), lambda: osp.tile([P, H, n, DH], F32, tag="ost", name="ost"))
+                src = st[("acc", b, t3, j)][:].rearrange("p (h d) -> p h d", h=H)
+                if eng == "S":
+                    nc.scalar.copy(out=ost[:, :, j - j0, :], in_=src)
                 else:
-                    nc.scalar.copy(out=ost[:, :, j - jbase, :], in_=src)
+                    nc.vector.tensor_copy(out=ost[:, :, j - j0, :], in_=src)
+            elif k == "st":
+                b, t3, j0, n = a
+                nc.sync.dma_start(
+                    out=outs[t3][b].rearrange("h (p j) d -> p h j d", j=J)[:, :, j0 : j0 + n, :],
+                    in_=st[("ost", b, t3, j0)][:],
+                )
+            else:
+                assert False, tok
 
-        def store(b, t3, j0, nj, ost):
-            nc.sync.dma_start(
-                out=outs[t3][b].rearrange("h (p j) d -> p h j d", j=J)[:, :, j0 : j0 + nj, :],
-                in_=ost[:],
-            )
-
-        pieces = []
-
-        def half_unit(b, t3, j0, v_every):
-            ost = osp.tile([P, H, G, DH], F32, tag="ost", name="osth")
-            passes(b, t3, range(j0, j0 + G), ost, j0, v_every)
-            store(b, t3, j0, G, ost)
-
-        def full_first(b, t3, v_every):
-            ost = osp.tile([P, H, J, DH], F32, tag="ost", name="ost")
-            state[("ost", b, t3)] = ost
-            passes(b, t3, range(0, G), ost, 0, v_every)
-
-        def full_second(b, t3, v_every):
-            ost = state[("ost", b, t3)]
-            passes(b, t3, range(G, J), ost, 0, v_every)
-            store(b, t3, 0, J, ost)
-
-        for b in range(NB):
-            for t3 in range(3):
-                if b in (1, 2):
-                    pieces.append((2 * b + 3, full_first, (b, t3)))
-                    pieces.append((2 * b + 3, full_second, (b, t3)))
-            for g in range(2):
-                for t3 in range(3):
-                    if b in (0, 3):
-                        pieces.append((2 * b + g + 2, half_unit, (b, t3, G * g)))
-
-        stats(0)
-        rsq(0)
-        norm(0)
-        flip(0)
-        wprep(0)
-        step = 1
-        nxt = 0
-        while nxt < len(pieces) or step <= NG:
-            if step < NG:
-                stats(step)
-                rsq(step)
-            if step <= NG:
-                affine(step - 1, 4)
-                regroup(step - 1)
-            if step == 1:
-                wprep(1)
-                wprep(2)
-            done = 0
-            while nxt < len(pieces) and done < 3 and pieces[nxt][0] <= step:
-                fn, args = pieces[nxt][1], pieces[nxt][2]
-                fn(*args, 2 if step > NG else 5)
-                done += 1
-                nxt += 1
-            if step < NG:
-                norm(step)
-                flip(step)
-            if step <= NG:
-                quant(step - 1)
-            step += 1
+        for tok in ORDER:
+            emit(tok)

@@ -16,314 +16,241 @@ ACT = mybir.ActivationFunctionType
 P = 128
 NB, SEQ, E, H, DH = 4, 1024, 512, 8, 64
 J = SEQ // P
+G = 4
+NG = NB * J // G
+THIRDS = 3
+PASSES = THIRDS * J
 EPS = 1e-5
-GROUPS = ((0, 0, 4), (0, 4, 4), (1, 0, 4), (1, 4, 4), (2, 0, 4), (2, 4, 4), (3, 0, 4), (3, 4, 4))
-XN_ENG = "VVVVVVVV"
-RG_ENG = "VVVVVVVV"
-PINNED = True
-ORDER = (
-    ("ident",), ("memset",), ("ldx", 0, 0, 4), ("ldwb",), ("ldw", 0), ("ldx", 0, 4, 4),
-    ("ldw", 1), ("ldw", 2), ("ldx", 1, 0, 8), ("ldx", 2, 0, 8), ("ldx", 3, 0, 8), ("bn", 0, 0),
-    ("wbT",), ("bn", 0, 1), ("bn", 0, 2), ("wt", 0, 0, 0), ("wt", 0, 0, 1), ("wt", 0, 0, 2),
-    ("bn", 0, 3), ("wt", 0, 0, 3), ("wt", 0, 1, 0), ("wt", 0, 1, 1), ("we", 0, 0, "S"), ("wt", 0, 1, 2),
-    ("wt", 0, 1, 3), ("ag", 0, 0), ("ag", 0, 1), ("ag", 0, 2), ("we", 0, 1, "S"), ("ag", 0, 3),
-    ("ve", 0), ("wbc",), ("bn", 1, 0), ("sq", 0), ("rc", 0), ("xn", 0, 0),
-    ("xn", 0, 1), ("tr", 0, 0, 0), ("tr", 0, 0, 1), ("tr", 0, 0, 2), ("xn", 0, 2), ("tr", 0, 0, 3),
-    ("tr", 0, 1, 0), ("tr", 0, 1, 1), ("xn", 0, 3), ("tr", 0, 1, 2), ("tr", 0, 1, 3), ("tr", 0, 2, 0),
-    ("tr", 0, 2, 1), ("wq", 0), ("tr", 0, 2, 2), ("tr", 0, 2, 3), ("tr", 0, 3, 0), ("tr", 0, 3, 1),
-    ("tr", 0, 3, 2), ("C", 0, 0, "S"), ("tr", 0, 3, 3), ("wt", 1, 0, 0), ("bn", 1, 1), ("wt", 1, 0, 1),
-    ("wt", 1, 0, 2), ("wt", 1, 0, 3), ("wt", 1, 1, 0), ("wt", 1, 1, 1), ("C", 0, 1, "S"), ("wt", 1, 1, 2),
-    ("wt", 1, 1, 3), ("bn", 1, 2), ("wt", 2, 0, 0), ("wt", 2, 0, 1), ("wt", 2, 0, 2), ("wt", 2, 0, 3),
-    ("wt", 2, 1, 0), ("C", 0, 2, "S"), ("wt", 2, 1, 1), ("wt", 2, 1, 2), ("bn", 1, 3), ("wt", 2, 1, 3),
-    ("C", 0, 3, "S"), ("ag", 1, 0), ("ag", 1, 1), ("ag", 1, 2), ("ag", 1, 3), ("ve", 1),
-    ("we", 1, 0, "V"), ("we", 1, 1, "S"), ("rg", 0), ("we", 2, 0, "S"), ("we", 2, 1, "S"), ("q", 0),
-    ("sq", 1), ("wq", 1), ("mx", 0, 0, 0), ("rc", 1), ("xn", 1, 0), ("mx", 0, 0, 1),
-    ("ev", 0, 0, 0, 0, 4, "S"), ("xn", 1, 1), ("mx", 0, 0, 2), ("xn", 1, 2), ("mx", 0, 0, 3), ("ev", 0, 0, 1, 0, 4, "S"),
-    ("xn", 1, 3), ("mx", 0, 1, 0), ("tr", 1, 0, 0), ("wq", 2), ("ev", 0, 0, 2, 0, 4, "S"), ("mx", 0, 1, 1),
-    ("ev", 0, 0, 3, 0, 4, "V"), ("tr", 1, 0, 1), ("ev", 0, 1, 0, 0, 4, "S"), ("mx", 0, 1, 2), ("bn", 2, 0), ("ev", 0, 1, 1, 0, 4, "S"),
-    ("st", 0, 0, 0, 4), ("mx", 0, 1, 3), ("tr", 1, 0, 2), ("bn", 2, 1), ("tr", 1, 0, 3), ("ev", 0, 1, 2, 0, 4, "S"),
-    ("tr", 1, 1, 0), ("tr", 1, 1, 1), ("tr", 1, 1, 2), ("tr", 1, 1, 3), ("tr", 1, 2, 0), ("tr", 1, 2, 1),
-    ("bn", 2, 2), ("tr", 1, 2, 2), ("ev", 0, 1, 3, 0, 4, "S"), ("tr", 1, 2, 3), ("tr", 1, 3, 0), ("tr", 1, 3, 1),
-    ("tr", 1, 3, 2), ("tr", 1, 3, 3), ("mx", 0, 2, 0), ("bn", 2, 3), ("C", 1, 0, "S"), ("st", 0, 1, 0, 4),
-    ("mx", 0, 2, 1), ("ag", 2, 0), ("C", 1, 1, "S"), ("ag", 2, 1), ("mx", 0, 2, 2), ("ag", 2, 2),
-    ("ag", 2, 3), ("ve", 2), ("mx", 0, 2, 3), ("bn", 3, 0), ("C", 1, 2, "S"), ("bn", 3, 1),
-    ("C", 1, 3, "S"), ("bn", 3, 2), ("ev", 0, 2, 0, 0, 4, "S"), ("rg", 1), ("ev", 0, 2, 1, 0, 4, "S"), ("ev", 0, 2, 2, 0, 4, "S"),
-    ("q", 1), ("ev", 0, 2, 3, 0, 4, "S"), ("bn", 3, 3), ("sq", 2), ("st", 0, 2, 0, 4), ("mx", 0, 0, 4),
-    ("rc", 2), ("mx", 0, 0, 5), ("xn", 2, 0), ("ev", 0, 0, 4, 4, 4, "S"), ("mx", 0, 0, 6), ("xn", 2, 1),
-    ("mx", 0, 0, 7), ("xn", 2, 2), ("ev", 0, 0, 5, 4, 4, "S"), ("mx", 0, 1, 4), ("xn", 2, 3), ("tr", 2, 0, 0),
-    ("ev", 0, 0, 6, 4, 4, "S"), ("ag", 3, 0), ("ag", 3, 1), ("mx", 0, 1, 5), ("ag", 3, 2), ("ag", 3, 3),
-    ("ve", 3), ("ev", 0, 0, 7, 4, 4, "V"), ("tr", 2, 0, 1), ("ev", 0, 1, 4, 4, 4, "S"), ("mx", 0, 1, 6), ("ev", 0, 1, 5, 4, 4, "V"),
-    ("st", 0, 0, 4, 4), ("sq", 3), ("mx", 0, 1, 7), ("ev", 0, 1, 6, 4, 4, "S"), ("tr", 2, 0, 2), ("rc", 3),
-    ("tr", 2, 0, 3), ("xn", 3, 0), ("tr", 2, 1, 0), ("tr", 2, 1, 1), ("ev", 0, 1, 7, 4, 4, "S"), ("tr", 2, 1, 2),
-    ("tr", 2, 1, 3), ("xn", 3, 1), ("tr", 2, 2, 0), ("tr", 2, 2, 1), ("tr", 2, 2, 2), ("xn", 3, 2),
-    ("tr", 2, 2, 3), ("tr", 2, 3, 0), ("tr", 2, 3, 1), ("st", 0, 1, 4, 4), ("tr", 2, 3, 2), ("C", 2, 0, "S"),
-    ("xn", 3, 3), ("tr", 2, 3, 3), ("mx", 0, 2, 4), ("C", 2, 1, "V"), ("mx", 0, 2, 5), ("C", 2, 2, "S"),
-    ("tr", 3, 0, 0), ("C", 2, 3, "V"), ("tr", 3, 0, 1), ("tr", 3, 1, 0), ("ev", 0, 2, 4, 4, 4, "S"), ("tr", 3, 1, 1),
-    ("tr", 3, 0, 2), ("tr", 3, 1, 2), ("tr", 3, 2, 0), ("rg", 2), ("tr", 3, 0, 3), ("tr", 3, 1, 3),
-    ("tr", 3, 2, 1), ("ev", 0, 2, 5, 4, 4, "S"), ("tr", 3, 2, 2), ("tr", 3, 2, 3), ("tr", 3, 3, 0), ("tr", 3, 3, 1),
-    ("tr", 3, 3, 2), ("tr", 3, 3, 3), ("mx", 0, 2, 6), ("C", 3, 0, "S"), ("q", 2), ("mx", 0, 2, 7),
-    ("C", 3, 1, "S"), ("C", 3, 2, "V"), ("C", 3, 3, "S"), ("mx", 1, 0, 0), ("ev", 0, 2, 6, 4, 4, "V"), ("mx", 1, 0, 1),
-    ("ev", 0, 2, 7, 4, 4, "S"), ("rg", 3), ("mx", 1, 0, 2), ("ev", 1, 0, 0, 0, 8, "S"), ("st", 0, 2, 4, 4), ("mx", 1, 0, 3),
-    ("ev", 1, 0, 1, 0, 8, "S"), ("q", 3), ("ev", 1, 0, 2, 0, 8, "S"), ("ev", 1, 0, 3, 0, 8, "V"), ("mx", 1, 0, 4), ("bn", 4, 0),
-    ("mx", 1, 0, 5), ("ev", 1, 0, 4, 0, 8, "S"), ("mx", 1, 0, 6), ("ev", 1, 0, 5, 0, 8, "V"), ("mx", 1, 0, 7), ("ev", 1, 0, 6, 0, 8, "S"),
-    ("mx", 1, 1, 0), ("ev", 1, 0, 7, 0, 8, "V"), ("mx", 1, 1, 1), ("ev", 1, 1, 0, 0, 8, "S"), ("mx", 1, 1, 2), ("bn", 4, 1),
-    ("st", 1, 0, 0, 8), ("mx", 1, 1, 3), ("ev", 1, 1, 1, 0, 8, "S"), ("mx", 1, 1, 4), ("bn", 4, 2), ("ev", 1, 1, 2, 0, 8, "S"),
-    ("mx", 1, 1, 5), ("bn", 4, 3), ("ev", 1, 1, 3, 0, 8, "S"), ("mx", 1, 1, 6), ("ag", 4, 0), ("ag", 4, 1),
-    ("ev", 1, 1, 4, 0, 8, "S"), ("ag", 4, 2), ("ag", 4, 3), ("mx", 1, 1, 7), ("ve", 4), ("bn", 5, 0),
-    ("ev", 1, 1, 5, 0, 8, "S"), ("mx", 1, 2, 0), ("bn", 5, 1), ("ev", 1, 1, 6, 0, 8, "S"), ("mx", 1, 2, 1), ("bn", 5, 2),
-    ("ev", 1, 1, 7, 0, 8, "S"), ("mx", 1, 2, 2), ("bn", 5, 3), ("ev", 1, 2, 0, 0, 8, "S"), ("st", 1, 1, 0, 8), ("mx", 1, 2, 3),
-    ("ag", 5, 0), ("ag", 5, 1), ("ag", 5, 2), ("ag", 5, 3), ("ev", 1, 2, 1, 0, 8, "S"), ("ve", 5),
-    ("mx", 1, 2, 4), ("ev", 1, 2, 2, 0, 8, "V"), ("ev", 1, 2, 3, 0, 8, "S"), ("mx", 1, 2, 5), ("ev", 1, 2, 4, 0, 8, "V"), ("mx", 1, 2, 6),
-    ("sq", 4), ("ev", 1, 2, 5, 0, 8, "S"), ("mx", 1, 2, 7), ("rc", 4), ("xn", 4, 0), ("xn", 4, 1),
-    ("ev", 1, 2, 6, 0, 8, "S"), ("tr", 4, 0, 0), ("xn", 4, 2), ("tr", 4, 0, 1), ("tr", 4, 0, 2), ("tr", 4, 0, 3),
-    ("tr", 4, 1, 0), ("xn", 4, 3), ("ev", 1, 2, 7, 0, 8, "S"), ("tr", 4, 1, 1), ("tr", 4, 1, 2), ("tr", 4, 1, 3),
-    ("tr", 4, 2, 0), ("bn", 6, 0), ("tr", 4, 2, 1), ("tr", 4, 2, 2), ("tr", 4, 2, 3), ("sq", 5),
-    ("tr", 4, 3, 0), ("st", 1, 2, 0, 8), ("tr", 4, 3, 1), ("tr", 4, 3, 2), ("C", 4, 0, "S"), ("rc", 5),
-    ("tr", 4, 3, 3), ("xn", 5, 0), ("xn", 5, 1), ("C", 4, 1, "S"), ("tr", 5, 0, 0), ("xn", 5, 2),
-    ("tr", 5, 1, 0), ("xn", 5, 3), ("tr", 5, 2, 0), ("C", 4, 2, "S"), ("tr", 5, 0, 1), ("C", 4, 3, "V"),
-    ("tr", 5, 1, 1), ("tr", 5, 2, 1), ("tr", 5, 3, 0), ("tr", 5, 3, 1), ("C", 5, 0, "S"), ("tr", 5, 0, 2),
-    ("rg", 4), ("tr", 5, 0, 3), ("tr", 5, 1, 2), ("tr", 5, 1, 3), ("tr", 5, 2, 2), ("tr", 5, 2, 3),
-    ("C", 5, 1, "S"), ("tr", 5, 3, 2), ("tr", 5, 3, 3), ("C", 5, 2, "S"), ("q", 4), ("C", 5, 3, "S"),
-    ("bn", 6, 1), ("mx", 2, 0, 0), ("rg", 5), ("mx", 2, 0, 1), ("ev", 2, 0, 0, 0, 8, "S"), ("mx", 2, 0, 2),
-    ("mx", 2, 0, 3), ("ev", 2, 0, 1, 0, 8, "S"), ("q", 5), ("ev", 2, 0, 2, 0, 8, "S"), ("ev", 2, 0, 3, 0, 8, "V"), ("mx", 2, 0, 4),
-    ("bn", 6, 2), ("mx", 2, 0, 5), ("ev", 2, 0, 4, 0, 8, "S"), ("mx", 2, 0, 6), ("ev", 2, 0, 5, 0, 8, "V"), ("mx", 2, 0, 7),
-    ("ev", 2, 0, 6, 0, 8, "S"), ("mx", 2, 1, 0), ("ev", 2, 0, 7, 0, 8, "V"), ("mx", 2, 1, 1), ("ev", 2, 1, 0, 0, 8, "S"), ("mx", 2, 1, 2),
-    ("bn", 6, 3), ("st", 2, 0, 0, 8), ("mx", 2, 1, 3), ("ev", 2, 1, 1, 0, 8, "S"), ("mx", 2, 1, 4), ("ag", 6, 0),
-    ("ag", 6, 1), ("ag", 6, 2), ("ev", 2, 1, 2, 0, 8, "S"), ("ag", 6, 3), ("mx", 2, 1, 5), ("ve", 6),
-    ("bn", 7, 0), ("ev", 2, 1, 3, 0, 8, "S"), ("mx", 2, 1, 6), ("bn", 7, 1), ("ev", 2, 1, 4, 0, 8, "S"), ("mx", 2, 1, 7),
-    ("bn", 7, 2), ("ev", 2, 1, 5, 0, 8, "S"), ("mx", 2, 2, 0), ("bn", 7, 3), ("ev", 2, 1, 6, 0, 8, "S"), ("mx", 2, 2, 1),
-    ("ag", 7, 0), ("ag", 7, 1), ("ag", 7, 2), ("ag", 7, 3), ("ev", 2, 1, 7, 0, 8, "S"), ("ve", 7),
-    ("mx", 2, 2, 2), ("ev", 2, 2, 0, 0, 8, "V"), ("ev", 2, 2, 1, 0, 8, "S"), ("st", 2, 1, 0, 8), ("mx", 2, 2, 3), ("ev", 2, 2, 2, 0, 8, "V"),
-    ("mx", 2, 2, 4), ("ev", 2, 2, 3, 0, 8, "S"), ("mx", 2, 2, 5), ("ev", 2, 2, 4, 0, 8, "V"), ("mx", 2, 2, 6), ("sq", 6),
-    ("ev", 2, 2, 5, 0, 8, "S"), ("mx", 2, 2, 7), ("rc", 6), ("xn", 6, 0), ("xn", 6, 1), ("ev", 2, 2, 6, 0, 8, "S"),
-    ("tr", 6, 0, 0), ("xn", 6, 2), ("tr", 6, 0, 1), ("tr", 6, 0, 2), ("tr", 6, 0, 3), ("tr", 6, 1, 0),
-    ("ev", 2, 2, 7, 0, 8, "S"), ("xn", 6, 3), ("tr", 6, 1, 1), ("tr", 6, 1, 2), ("tr", 6, 1, 3), ("tr", 6, 2, 0),
-    ("tr", 6, 2, 1), ("tr", 6, 2, 2), ("tr", 6, 2, 3), ("sq", 7), ("tr", 6, 3, 0), ("st", 2, 2, 0, 8),
-    ("tr", 6, 3, 1), ("rc", 7), ("tr", 6, 3, 2), ("C", 6, 0, "S"), ("xn", 7, 0), ("tr", 6, 3, 3),
-    ("xn", 7, 1), ("C", 6, 1, "S"), ("xn", 7, 2), ("tr", 7, 0, 0), ("tr", 7, 1, 0), ("xn", 7, 3),
-    ("tr", 7, 2, 0), ("C", 6, 2, "S"), ("C", 6, 3, "V"), ("tr", 7, 0, 1), ("tr", 7, 1, 1), ("tr", 7, 2, 1),
-    ("tr", 7, 3, 0), ("tr", 7, 3, 1), ("C", 7, 0, "V"), ("C", 7, 1, "S"), ("tr", 7, 0, 2), ("tr", 7, 0, 3),
-    ("tr", 7, 1, 2), ("tr", 7, 1, 3), ("tr", 7, 2, 2), ("tr", 7, 2, 3), ("rg", 6), ("tr", 7, 3, 2),
-    ("tr", 7, 3, 3), ("C", 7, 2, "S"), ("C", 7, 3, "S"), ("q", 6), ("rg", 7), ("mx", 3, 0, 0),
-    ("mx", 3, 0, 1), ("ev", 3, 0, 0, 0, 8, "S"), ("mx", 3, 0, 2), ("q", 7), ("mx", 3, 0, 3), ("ev", 3, 0, 1, 0, 8, "S"),
-    ("ev", 3, 0, 2, 0, 8, "V"), ("ev", 3, 0, 3, 0, 8, "S"), ("mx", 3, 0, 4), ("mx", 3, 0, 5), ("ev", 3, 0, 4, 0, 8, "V"), ("mx", 3, 0, 6),
-    ("ev", 3, 0, 5, 0, 8, "S"), ("mx", 3, 0, 7), ("ev", 3, 0, 6, 0, 8, "V"), ("mx", 3, 1, 0), ("ev", 3, 0, 7, 0, 8, "S"), ("mx", 3, 1, 1),
-    ("ev", 3, 1, 0, 0, 8, "V"), ("mx", 3, 1, 2), ("ev", 3, 1, 1, 0, 8, "S"), ("st", 3, 0, 0, 8), ("mx", 3, 1, 3), ("ev", 3, 1, 2, 0, 8, "V"),
-    ("mx", 3, 1, 4), ("ev", 3, 1, 3, 0, 8, "S"), ("mx", 3, 1, 5), ("ev", 3, 1, 4, 0, 8, "V"), ("mx", 3, 1, 6), ("ev", 3, 1, 5, 0, 8, "S"),
-    ("mx", 3, 1, 7), ("ev", 3, 1, 6, 0, 8, "V"), ("mx", 3, 2, 0), ("ev", 3, 1, 7, 0, 8, "S"), ("mx", 3, 2, 1), ("ev", 3, 2, 0, 0, 8, "V"),
-    ("mx", 3, 2, 2), ("ev", 3, 2, 1, 0, 8, "S"), ("st", 3, 1, 0, 8), ("mx", 3, 2, 3), ("ev", 3, 2, 2, 0, 8, "V"), ("mx", 3, 2, 4),
-    ("ev", 3, 2, 3, 0, 8, "S"), ("mx", 3, 2, 5), ("ev", 3, 2, 4, 0, 8, "V"), ("mx", 3, 2, 6), ("ev", 3, 2, 5, 0, 8, "S"), ("mx", 3, 2, 7),
-    ("ev", 3, 2, 6, 0, 8, "V"), ("ev", 3, 2, 7, 0, 8, "S"), ("st", 3, 2, 0, 8),
-)
+
+AFTER_STATS_A = 7
+AFTER_STATS_B = 6
+BEFORE_FLIP_A = 3
+BEFORE_FLIP_B = 4
 
 
 def tile_selfattention_pa_t_kernel(tc, inputs, ln_w, ln_b, w_qkv, out_0, out_1, out_2):
     nc = tc.nc
     outs = (out_0, out_1, out_2)
-    ng = len(GROUPS)
     with ExitStack() as ctx:
         keep = ctx.enter_context(tc.tile_pool(name="keep", bufs=1))
         wgp = ctx.enter_context(tc.tile_pool(name="wgp", bufs=2))
-        sp = ctx.enter_context(tc.tile_pool(name="sp", bufs=8))
-        xnp = ctx.enter_context(tc.tile_pool(name="xnp", bufs=8))
+        sp = ctx.enter_context(tc.tile_pool(name="sp", bufs=4))
+        xnp = ctx.enter_context(tc.tile_pool(name="xnp", bufs=2 * G))
         plp = ctx.enter_context(tc.tile_pool(name="plp", bufs=2))
         grp = ctx.enter_context(tc.tile_pool(name="grp", bufs=2))
         osp = ctx.enter_context(tc.tile_pool(name="osp", bufs=7))
         xtp = ctx.enter_context(tc.psum_pool(name="xtp", bufs=1))
         accp = ctx.enter_context(tc.psum_pool(name="accp", bufs=4))
-        if PINNED:
-            ctx.enter_context(tc.manual_schedule())
+        ctx.enter_context(tc.manual_schedule())
 
         wb_raw = keep.tile([P, 2 * P], BF16, name="wb_raw")
         one_t = keep.tile([P, 1], F32, name="one_t")
         junk = keep.tile([P, 1], F32, name="junk")
         ident = keep.tile([P, P], F32, name="ident")
         x_sb = [keep.tile([P, J, E], BF16, name="x%d" % b) for b in range(NB)]
-        w_sb = keep.tile([P, 12, E], BF16, name="w_sb")
-        xv = [inputs[b].rearrange("(p j) k -> p j k", j=J) for b in range(NB)]
-        wcodes = keep.tile([P, 1536], U32, name="wcodes", align_bytes=64)
-        wscales = keep.tile([P, 1536], U8, name="wscales", align_bytes=64)
-        xc = [keep.tile([P, P * GROUPS[g][2]], U32, name="xc%d" % g, align_bytes=64) for g in range(ng)]
-        xs = [keep.tile([P, P * GROUPS[g][2]], U8, name="xs%d" % g, align_bytes=64) for g in range(ng)]
+        w_sb = keep.tile([P, THIRDS * 4, E], BF16, name="w_sb")
+        wcodes = keep.tile([P, THIRDS * E], U32, name="wcodes", align_bytes=64)
+        wscales = keep.tile([P, THIRDS * E], U8, name="wscales", align_bytes=64)
+        xc = [keep.tile([P, G * P], U32, name="xc%d" % g, align_bytes=64) for g in range(NG)]
+        xs = [keep.tile([P, G * P], U8, name="xs%d" % g, align_bytes=64) for g in range(NG)]
         wbc = keep.tile([P, 8], F32, name="wbc")
+        xv = [inputs[b].rearrange("(p j) k -> p j k", j=J) for b in range(NB)]
         st = {}
 
-        def group_of(b, j):
-            for g in range(ng):
-                if GROUPS[g][0] == b and GROUPS[g][1] <= j < GROUPS[g][1] + GROUPS[g][2]:
-                    return g
-            return -1
+        def x_tile(g, i):
+            return x_sb[g // 2][:, G * (g % 2) + i, :]
 
-        def get(key, make):
-            if key not in st:
-                st[key] = make()
-            return st[key]
+        def load_w(t):
+            nc.sync.dma_start(
+                out=w_sb[:, 4 * t : 4 * t + 4, :],
+                in_=w_qkv[E * t : E * t + E, :].rearrange("(r p) k -> p r k", p=P),
+            )
 
-        def emit(tok):
-            k = tok[0]
-            a = [v for v in tok[1:] if v not in ("S", "V")]
-            eng = tok[-1]
-            if k == "ident":
-                make_identity(nc, ident[:])
-            elif k == "memset":
-                nc.vector.memset(wb_raw[:], 0.0)
-                nc.vector.memset(one_t[:], 1.0)
-                nc.scalar.activation(out=junk[:], in_=one_t[:], func=ACT.Sqrt)
-            elif k == "ldwb":
-                nc.sync.dma_start(out=wb_raw[0:2, :], in_=ln_w.rearrange("(u c) -> u c", u=2))
-                nc.sync.dma_start(out=wb_raw[2:4, :], in_=ln_b.rearrange("(u c) -> u c", u=2))
-            elif k == "ldw":
-                t = a[0]
-                nc.sync.dma_start(
-                    out=w_sb[:, 4 * t : 4 * t + 4, :],
-                    in_=w_qkv[512 * t : 512 * t + 512, :].rearrange("(r p) k -> p r k", p=P),
+        def gain_bias():
+            wbT = accp.tile([P, 512], F32, tag="acc", name="wbT")
+            nc.tensor.transpose(wbT[:, 0:P], wb_raw[:].bitcast(F32), ident[:])
+            nc.vector.tensor_copy(out=wbc[:], in_=wbT[:, 0:4].bitcast(BF16))
+
+        def w_flip(t):
+            wg = wgp.tile([P, E, 2], F32, name="wg", align_bytes=64)
+            st[("wg", t)] = wg
+            for half in range(2):
+                wt = accp.tile([P, 2, 2 * P], F32, tag="acc", name="wt")
+                for rr in range(2):
+                    words = w_sb[:, 4 * t + 2 * half + rr, :].bitcast(F32)
+                    for u in range(2):
+                        nc.tensor.transpose(wt[:, u, P * rr : P * rr + P], words[:, P * u : P * u + P], ident[:])
+                nc.scalar.copy(
+                    out=wg[:, 2 * P * half : 2 * P * half + 2 * P, :], in_=wt[:].rearrange("p u n -> p n u")
                 )
-            elif k == "ldx":
-                b, j0, n = a
-                nc.sync.dma_start(out=x_sb[b][:, j0 : j0 + n, :], in_=xv[b][:, j0 : j0 + n, :])
-            elif k == "wbT":
-                wbT = accp.tile([P, 512], F32, tag="acc", name="wbT")
-                st["wbT"] = wbT
-                nc.tensor.transpose(wbT[:, 0:P], wb_raw[:].bitcast(F32), ident[:])
-            elif k == "wbc":
-                nc.vector.tensor_copy(out=wbc[:], in_=st["wbT"][:, 0:4].bitcast(BF16))
-            elif k == "wt":
-                t, half, i = a
-                wt = get(("wt", t, half), lambda: accp.tile([P, 2, 256], F32, tag="acc", name="wt"))
-                rr, u = i // 2, i % 2
-                words = w_sb[:, 4 * t + 2 * half + rr, :].bitcast(F32)
-                nc.tensor.transpose(wt[:, u, P * rr : P * rr + P], words[:, P * u : P * u + P], ident[:])
-            elif k == "we":
-                t, half = a
-                wg = get(("wg", t), lambda: wgp.tile([P, 512, 2], F32, name="wg", align_bytes=64))
-                dst = wg[:, 256 * half : 256 * half + 256, :]
-                src = st[("wt", t, half)][:].rearrange("p u n -> p n u")
-                if eng == "S":
-                    nc.scalar.copy(out=dst, in_=src)
-                else:
-                    nc.vector.tensor_copy(out=dst, in_=src)
-            elif k == "wq":
-                t = a[0]
-                nc.vector.quantize_mx(
-                    out=wcodes[:, 512 * t : 512 * t + 512].bitcast(FP8X4),
-                    scales=wscales[:, 512 * t : 512 * t + 512],
-                    in_=st[("wg", t)][:].rearrange("p n u -> p (n u)").bitcast(BF16),
-                )
-            elif k == "bn":
-                g, i = a
-                b, j0, n = GROUPS[g]
-                sts = get(("st", g), lambda: sp.tile([P, 4, 6], F32, name="sts"))
-                nc.vector.bn_stats(out=sts[:, i, :], in_=x_sb[b][:, j0 + i, :])
-            elif k == "ag":
-                g, i = a
-                mv = get(("mv", g), lambda: sp.tile([P, 4, 2], F32, name="mv"))
-                nc.vector.bn_aggr(out=mv[:, i, :], in_=st[("st", g)][:, i, :])
-            elif k == "ve":
-                g = a[0]
-                n = GROUPS[g][2]
-                ve = sp.tile([P, 4, 1], F32, name="ve")
+
+        def w_quant(t):
+            nc.vector.quantize_mx(
+                out=wcodes[:, E * t : E * t + E].bitcast(FP8X4),
+                scales=wscales[:, E * t : E * t + E],
+                in_=st[("wg", t)][:].rearrange("p n u -> p (n u)").bitcast(BF16),
+            )
+
+        def stats(g, first=0, last=G):
+            if first == 0:
+                st[("sts", g)] = sp.tile([P, G, 6], F32, name="sts")
+                st[("mv", g)] = sp.tile([P, G, 2], F32, name="mv")
+            sts, mv = st[("sts", g)], st[("mv", g)]
+            for i in range(first, last):
+                nc.vector.bn_stats(out=sts[:, i, :], in_=x_tile(g, i))
+                nc.vector.bn_aggr(out=mv[:, i, :], in_=sts[:, i, :])
+            if last == G:
+                ve = sp.tile([P, G, 1], F32, name="ve")
                 st[("ve", g)] = ve
-                nc.vector.tensor_scalar_add(out=ve[:, 0:n, :], in0=st[("mv", g)][:, 0:n, 1:2], scalar1=EPS)
-            elif k == "sq":
-                g = a[0]
-                n = GROUPS[g][2]
-                std = sp.tile([P, 4, 1], F32, name="std")
-                st[("std", g)] = std
-                nc.scalar.activation(out=std[:, 0:n, :], in_=st[("ve", g)][:, 0:n, :], func=ACT.Sqrt)
-            elif k == "rc":
-                g = a[0]
-                n = GROUPS[g][2]
-                rstd = sp.tile([P, 4, 1], F32, name="rstd")
-                st[("rstd", g)] = rstd
-                nc.vector.reciprocal(out=rstd[:, 0:n, :], in_=st[("std", g)][:, 0:n, :])
-                if XN_ENG[g] == "G":
-                    nmu = sp.tile([P, 4, 1], F32, name="nmu")
-                    st[("nmu", g)] = nmu
-                    nc.vector.tensor_scalar_mul(out=nmu[:, 0:n, :], in0=st[("mv", g)][:, 0:n, 0:1], scalar1=-1.0)
-            elif k == "xn":
-                g, i = a
-                b, j0, n = GROUPS[g]
+                nc.vector.tensor_scalar_add(out=ve[:], in0=mv[:, :, 1:2], scalar1=EPS)
+
+        def root(g):
+            std = sp.tile([P, G, 1], F32, name="std")
+            st[("std", g)] = std
+            nc.scalar.activation(out=std[:], in_=st[("ve", g)][:], func=ACT.Sqrt)
+
+        def normalise(g):
+            mv = st[("mv", g)]
+            rstd = sp.tile([P, G, 1], F32, name="rstd")
+            nc.vector.reciprocal(out=rstd[:], in_=st[("std", g)][:])
+            for i in range(G):
                 xn = xnp.tile([P, E], F32, name="xn")
                 st[("xn", g, i)] = xn
-                dst = xn[:].rearrange("p (u e q) -> p u e q", u=2, e=2)
-                src = x_sb[b][:, j0 + i, :].rearrange("p (u q e) -> p u e q", u=2, e=2)
-                if XN_ENG[g] == "G":
-                    nc.gpsimd.tensor_scalar(
-                        out=dst, in0=src, scalar1=st[("nmu", g)][:, i, 0:1], scalar2=st[("rstd", g)][:, i, 0:1],
-                        op0=ALU.add, op1=ALU.mult,
+                nc.vector.tensor_scalar(
+                    out=xn[:].rearrange("p (u e q) -> p u e q", u=2, e=2),
+                    in0=x_tile(g, i).rearrange("p (u q e) -> p u e q", u=2, e=2),
+                    scalar1=mv[:, i, 0:1],
+                    scalar2=rstd[:, i, 0:1],
+                    op0=ALU.subtract,
+                    op1=ALU.mult,
+                )
+
+        def flip(g):
+            xts = [xtp.tile([P, G * P], F32, name="xt%d" % t) for t in range(4)]
+            st[("xt", g)] = xts
+            for i in range(G):
+                for t in range(4):
+                    nc.tensor.transpose(
+                        xts[t][:, P * i : P * i + P], st[("xn", g, i)][:, P * t : P * t + P], ident[:]
                     )
-                else:
-                    nc.vector.tensor_scalar(
-                        out=dst, in0=src, scalar1=st[("mv", g)][:, i, 0:1], scalar2=st[("rstd", g)][:, i, 0:1],
-                        op0=ALU.subtract, op1=ALU.mult,
-                    )
-            elif k == "tr":
-                g, i, t = a
-                xt = get(("xt", g, t), lambda: xtp.tile([P, 512], F32, name="xt%d" % t))
-                nc.tensor.transpose(xt[:, P * i : P * i + P], st[("xn", g, i)][:, P * t : P * t + P], ident[:])
-            elif k == "C":
-                g, t = a
-                w = P * GROUPS[g][2]
-                pl = get(("pl", g), lambda: plp.tile([P, 4, 512], BF16, name="pl"))
-                if eng == "S":
+
+        def affine(g, on_scalar):
+            pl = plp.tile([P, 4, G * P], BF16, name="pl")
+            st[("pl", g)] = pl
+            for t in range(4):
+                bank = st[("xt", g)][t]
+                if t < on_scalar:
                     nc.scalar.activation(
-                        out=pl[:, t, 0:w], in_=st[("xt", g, t)][:, 0:w], func=ACT.Identity,
+                        out=pl[:, t, :], in_=bank[:], func=ACT.Identity,
                         bias=wbc[:, 4 + t : 5 + t], scale=wbc[:, t : t + 1],
                     )
                 else:
                     nc.vector.tensor_scalar(
-                        out=pl[:, t, 0:w], in0=st[("xt", g, t)][:, 0:w],
+                        out=pl[:, t, :], in0=bank[:],
                         scalar1=wbc[:, t : t + 1], scalar2=wbc[:, 4 + t : 5 + t], op0=ALU.mult, op1=ALU.add,
                     )
-            elif k == "rg":
-                g = a[0]
-                w = P * GROUPS[g][2]
-                gr = grp.tile([P, 512, 4], BF16, name="gr", align_bytes=64)
-                st[("gr", g)] = gr
-                dst = gr[:, 0:w, :].rearrange("p (c i) t -> p c t i", i=4)
-                src = st[("pl", g)][:, :, 0:w].rearrange("p t (c i) -> p c t i", i=4)
-                if RG_ENG[g] == "G":
-                    nc.gpsimd.tensor_scalar(out=dst, in0=src, scalar1=1.0, scalar2=0.0, op0=ALU.mult, op1=ALU.add)
-                else:
-                    nc.vector.tensor_copy(out=dst, in_=src)
-            elif k == "q":
-                g = a[0]
-                w = P * GROUPS[g][2]
-                nc.vector.quantize_mx(
-                    out=xc[g][:].bitcast(FP8X4), scales=xs[g][:],
-                    in_=st[("gr", g)][:, 0:w, :].rearrange("p c t -> p (c t)"),
-                )
-            elif k == "mx":
-                b, t3, j = a
-                g = group_of(b, j)
-                i = j - GROUPS[g][1]
-                acc = accp.tile([P, 512], F32, tag="acc", name="acc")
-                st[("acc", b, t3, j)] = acc
+
+        def regroup(g):
+            gr = grp.tile([P, G * P, 4], BF16, name="gr", align_bytes=64)
+            st[("gr", g)] = gr
+            nc.vector.tensor_copy(
+                out=gr[:].rearrange("p (c i) t -> p c t i", i=4),
+                in_=st[("pl", g)][:].rearrange("p t (c i) -> p c t i", i=4),
+            )
+
+        def quant(g):
+            nc.vector.quantize_mx(
+                out=xc[g][:].bitcast(FP8X4), scales=xs[g][:], in_=st[("gr", g)][:].rearrange("p c t -> p (c t)")
+            )
+
+        done = [0]
+
+        def project(count, on_vector):
+            for i in range(count):
+                b, t3, j = done[0] // PASSES, (done[0] % PASSES) // J, done[0] % J
+                done[0] += 1
+                if j == 0:
+                    st["ost"] = osp.tile([P, H, J, DH], F32, name="ost")
+                ost = st["ost"]
+                g, c = 2 * b + j // G, P * (j % G)
+                acc = accp.tile([P, E], F32, tag="acc", name="acc")
                 nc.tensor.matmul_mx(
                     out=acc[:],
-                    lhsT=xc[g][:, P * i : P * i + P].bitcast(FP8X4),
-                    lhsT_scale=xs[g][:, P * i : P * i + P],
-                    rhs=wcodes[:, 512 * t3 : 512 * t3 + 512].bitcast(FP8X4),
-                    rhs_scale=wscales[:, 512 * t3 : 512 * t3 + 512],
+                    lhsT=xc[g][:, c : c + P].bitcast(FP8X4),
+                    lhsT_scale=xs[g][:, c : c + P],
+                    rhs=wcodes[:, E * t3 : E * t3 + E].bitcast(FP8X4),
+                    rhs_scale=wscales[:, E * t3 : E * t3 + E],
                     start=True,
                     stop=True,
                 )
-            elif k == "ev":
-                b, t3, j, j0, n = a
-                ost = get(("ost", b, t3, j0), lambda: osp.tile([P, H, n, DH], F32, tag="ost", name="ost"))
-                src = st[("acc", b, t3, j)][:].rearrange("p (h d) -> p h d", h=H)
-                if eng == "S":
-                    nc.scalar.copy(out=ost[:, :, j - j0, :], in_=src)
+                heads = acc[:].rearrange("p (h d) -> p h d", h=H)
+                if on_vector(i):
+                    nc.vector.tensor_copy(out=ost[:, :, j, :], in_=heads)
                 else:
-                    nc.vector.tensor_copy(out=ost[:, :, j - j0, :], in_=src)
-            elif k == "st":
-                b, t3, j0, n = a
-                nc.sync.dma_start(
-                    out=outs[t3][b].rearrange("h (p j) d -> p h j d", j=J)[:, :, j0 : j0 + n, :],
-                    in_=st[("ost", b, t3, j0)][:],
-                )
-            else:
-                assert False, tok
+                    nc.scalar.copy(out=ost[:, :, j, :], in_=heads)
+                if j == J - 1:
+                    nc.sync.dma_start(out=outs[t3][b].rearrange("h (p j) d -> p h j d", j=J), in_=ost[:])
 
-        for tok in ORDER:
-            emit(tok)
+        def never(i):
+            return False
+
+        nc.vector.memset(wb_raw[:], 0.0)
+        nc.vector.memset(one_t[:], 1.0)
+        nc.scalar.activation(out=junk[:], in_=one_t[:], func=ACT.Sqrt)
+        make_identity(nc, ident[:])
+        nc.sync.dma_start(out=x_sb[0][:, 0:G, :], in_=xv[0][:, 0:G, :])
+        nc.sync.dma_start(out=wb_raw[0:2, :], in_=ln_w.rearrange("(u c) -> u c", u=2))
+        nc.sync.dma_start(out=wb_raw[2:4, :], in_=ln_b.rearrange("(u c) -> u c", u=2))
+        load_w(0)
+        nc.sync.dma_start(out=x_sb[0][:, G:J, :], in_=xv[0][:, G:J, :])
+        load_w(1)
+        load_w(2)
+        for b in range(1, NB):
+            nc.sync.dma_start(out=x_sb[b][:], in_=xv[b])
+
+        stats(0)
+        root(0)
+        gain_bias()
+        w_flip(0)
+        stats(1, 0, 1)
+        normalise(0)
+        flip(0)
+        stats(1, 1, G)
+        root(1)
+        affine(0, 2)
+        normalise(1)
+        regroup(0)
+        flip(1)
+        w_quant(0)
+        quant(0)
+        affine(1, 3)
+        w_flip(1)
+        w_flip(2)
+        regroup(1)
+        quant(1)
+        w_quant(1)
+
+        for b in range(NB - 1):
+            ga, gb = 2 * b + 2, 2 * b + 3
+            stats(ga)
+            if b == 0:
+                w_quant(2)
+            project(AFTER_STATS_A, never)
+            root(ga)
+            stats(gb)
+            project(AFTER_STATS_B, never)
+            root(gb)
+            normalise(ga)
+            normalise(gb)
+            project(BEFORE_FLIP_A, never)
+            flip(ga)
+            affine(ga, 2)
+            regroup(ga)
+            project(BEFORE_FLIP_B, lambda i: i == BEFORE_FLIP_B - 1)
+            flip(gb)
+            affine(gb, 2)
+            quant(ga)
+            regroup(gb)
+            project(PASSES - AFTER_STATS_A - AFTER_STATS_B - BEFORE_FLIP_A - BEFORE_FLIP_B, never)
+            quant(gb)
+        project(PASSES, lambda i: i % 2 == 1)

@@ -22,10 +22,7 @@ THIRDS = 3
 PASSES = THIRDS * J
 EPS = 1e-5
 
-AFTER_STATS_A = 7
-AFTER_STATS_B = 6
-BEFORE_FLIP_A = 3
-BEFORE_FLIP_B = 4
+VECTOR_SHARE = 4
 
 
 def tile_selfattention_pa_t_kernel(tc, inputs, ln_w, ln_b, w_qkv, out_0, out_1, out_2):
@@ -41,7 +38,6 @@ def tile_selfattention_pa_t_kernel(tc, inputs, ln_w, ln_b, w_qkv, out_0, out_1, 
         osp = ctx.enter_context(tc.tile_pool(name="osp", bufs=7))
         xtp = ctx.enter_context(tc.psum_pool(name="xtp", bufs=1))
         accp = ctx.enter_context(tc.psum_pool(name="accp", bufs=4))
-        ctx.enter_context(tc.manual_schedule())
 
         wb_raw = keep.tile([P, 2 * P], BF16, name="wb_raw")
         one_t = keep.tile([P, 1], F32, name="one_t")
@@ -98,6 +94,7 @@ def tile_selfattention_pa_t_kernel(tc, inputs, ln_w, ln_b, w_qkv, out_0, out_1, 
             sts, mv = st[("sts", g)], st[("mv", g)]
             for i in range(first, last):
                 nc.vector.bn_stats(out=sts[:, i, :], in_=x_tile(g, i))
+            for i in range(first, last):
                 nc.vector.bn_aggr(out=mv[:, i, :], in_=sts[:, i, :])
             if last == G:
                 ve = sp.tile([P, G, 1], F32, name="ve")
@@ -128,11 +125,12 @@ def tile_selfattention_pa_t_kernel(tc, inputs, ln_w, ln_b, w_qkv, out_0, out_1, 
         def flip(g):
             xts = [xtp.tile([P, G * P], F32, name="xt%d" % t) for t in range(4)]
             st[("xt", g)] = xts
-            for i in range(G):
-                for t in range(4):
-                    nc.tensor.transpose(
-                        xts[t][:, P * i : P * i + P], st[("xn", g, i)][:, P * t : P * t + P], ident[:]
-                    )
+            with tc.high_priority():
+                for i in range(G):
+                    for t in range(4):
+                        nc.tensor.transpose(
+                            xts[t][:, P * i : P * i + P], st[("xn", g, i)][:, P * t : P * t + P], ident[:]
+                        )
 
         def affine(g, on_scalar):
             pl = plp.tile([P, 4, G * P], BF16, name="pl")
@@ -191,9 +189,6 @@ def tile_selfattention_pa_t_kernel(tc, inputs, ln_w, ln_b, w_qkv, out_0, out_1, 
                 if j == J - 1:
                     nc.sync.dma_start(out=outs[t3][b].rearrange("h (p j) d -> p h j d", j=J), in_=ost[:])
 
-        def never(i):
-            return False
-
         nc.vector.memset(wb_raw[:], 0.0)
         nc.vector.memset(one_t[:], 1.0)
         nc.scalar.activation(out=junk[:], in_=one_t[:], func=ACT.Sqrt)
@@ -208,49 +203,30 @@ def tile_selfattention_pa_t_kernel(tc, inputs, ln_w, ln_b, w_qkv, out_0, out_1, 
         for b in range(1, NB):
             nc.sync.dma_start(out=x_sb[b][:], in_=xv[b])
 
+        gain_bias()
         stats(0)
         root(0)
-        gain_bias()
-        w_flip(0)
-        stats(1, 0, 1)
         normalise(0)
         flip(0)
-        stats(1, 1, G)
-        root(1)
-        affine(0, 2)
-        normalise(1)
-        regroup(0)
-        flip(1)
+        w_flip(0)
         w_quant(0)
-        quant(0)
-        affine(1, 3)
-        w_flip(1)
-        w_flip(2)
-        regroup(1)
-        quant(1)
-        w_quant(1)
-
-        for b in range(NB - 1):
-            ga, gb = 2 * b + 2, 2 * b + 3
-            stats(ga)
-            if b == 0:
+        for s in range(1, NG + 3):
+            if s < NG:
+                stats(s)
+                root(s)
+            if s <= NG:
+                affine(s - 1, 4 if s <= 2 else 2)
+                regroup(s - 1)
+            if s == 1:
+                w_flip(1)
+                w_quant(1)
+                w_flip(2)
                 w_quant(2)
-            project(AFTER_STATS_A, never)
-            root(ga)
-            stats(gb)
-            project(AFTER_STATS_B, never)
-            root(gb)
-            normalise(ga)
-            normalise(gb)
-            project(BEFORE_FLIP_A, never)
-            flip(ga)
-            affine(ga, 2)
-            regroup(ga)
-            project(BEFORE_FLIP_B, lambda i: i == BEFORE_FLIP_B - 1)
-            flip(gb)
-            affine(gb, 2)
-            quant(ga)
-            regroup(gb)
-            project(PASSES - AFTER_STATS_A - AFTER_STATS_B - BEFORE_FLIP_A - BEFORE_FLIP_B, never)
-            quant(gb)
-        project(PASSES, lambda i: i % 2 == 1)
+            if s >= 3:
+                share = VECTOR_SHARE if s <= NG else 2
+                project(PASSES // 2, lambda i: i % share == share - 1)
+            if s < NG:
+                normalise(s)
+                flip(s)
+            if s <= NG:
+                quant(s - 1)

@@ -165,10 +165,16 @@ def tile_selfattention_pa_t_kernel(tc, inputs, ln_w, ln_b, w_qkv, out_0, out_1, 
 
         def project(count, on_vector):
             for i in range(count):
-                b, t3, j = done[0] // PASSES, (done[0] % PASSES) // J, done[0] % J
+                b, n = done[0] // PASSES, done[0] % PASSES
                 done[0] += 1
-                if j == 0:
-                    st["ost"] = osp.tile([P, H, J, DH], F32, name="ost")
+                if b == 0:
+                    t3, j0, nj = (n % (PASSES // 2)) // G, G * (n // (PASSES // 2)), G
+                    j = j0 + n % G
+                else:
+                    t3, j0, nj = n // J, 0, J
+                    j = n % J
+                if j == j0:
+                    st["ost"] = osp.tile([P, H, nj, DH], F32, tag="ost", name="ost")
                 ost = st["ost"]
                 g, c = 2 * b + j // G, P * (j % G)
                 acc = accp.tile([P, E], F32, tag="acc", name="acc")
@@ -183,11 +189,13 @@ def tile_selfattention_pa_t_kernel(tc, inputs, ln_w, ln_b, w_qkv, out_0, out_1, 
                 )
                 heads = acc[:].rearrange("p (h d) -> p h d", h=H)
                 if on_vector(i):
-                    nc.vector.tensor_copy(out=ost[:, :, j, :], in_=heads)
+                    nc.vector.tensor_copy(out=ost[:, :, j - j0, :], in_=heads)
                 else:
-                    nc.scalar.copy(out=ost[:, :, j, :], in_=heads)
-                if j == J - 1:
-                    nc.sync.dma_start(out=outs[t3][b].rearrange("h (p j) d -> p h j d", j=J), in_=ost[:])
+                    nc.scalar.copy(out=ost[:, :, j - j0, :], in_=heads)
+                if j == j0 + nj - 1:
+                    nc.sync.dma_start(
+                        out=outs[t3][b].rearrange("h (p j) d -> p h j d", j=J)[:, :, j0 : j0 + nj, :], in_=ost[:]
+                    )
 
         nc.vector.memset(wb_raw[:], 0.0)
         nc.vector.memset(one_t[:], 1.0)
@@ -211,22 +219,21 @@ def tile_selfattention_pa_t_kernel(tc, inputs, ln_w, ln_b, w_qkv, out_0, out_1, 
         w_flip(0)
         w_quant(0)
         for s in range(1, NG + 3):
-            if s < NG:
-                stats(s)
-                root(s)
             if s <= NG:
                 affine(s - 1, 4 if s <= 2 else 2)
                 regroup(s - 1)
+            if s in (2, 3) or s >= 5:
+                share = VECTOR_SHARE if s <= NG else 2
+                project(PASSES // 2, lambda i: i % share == share - 1)
+            if s < NG:
+                stats(s)
+                root(s)
+                normalise(s)
+                flip(s)
+            if s <= NG:
+                quant(s - 1)
             if s == 1:
                 w_flip(1)
                 w_quant(1)
                 w_flip(2)
                 w_quant(2)
-            if s >= 3:
-                share = VECTOR_SHARE if s <= NG else 2
-                project(PASSES // 2, lambda i: i % share == share - 1)
-            if s < NG:
-                normalise(s)
-                flip(s)
-            if s <= NG:
-                quant(s - 1)

@@ -23,6 +23,7 @@ PASSES = THIRDS * J
 EPS = 1e-5
 
 VECTOR_SHARE = 4
+STORE_HEADS = 4
 
 
 def tile_selfattention_pa_t_kernel(tc, inputs, ln_w, ln_b, w_qkv, out_0, out_1, out_2):
@@ -193,9 +194,11 @@ def tile_selfattention_pa_t_kernel(tc, inputs, ln_w, ln_b, w_qkv, out_0, out_1, 
                 else:
                     nc.scalar.copy(out=ost[:, :, j - j0, :], in_=heads)
                 if j == j0 + nj - 1:
-                    nc.sync.dma_start(
-                        out=outs[t3][b].rearrange("h (p j) d -> p h j d", j=J)[:, :, j0 : j0 + nj, :], in_=ost[:]
-                    )
+                    rows = outs[t3][b].rearrange("h (p j) d -> p h j d", j=J)
+                    for h0 in range(0, H, STORE_HEADS):
+                        nc.sync.dma_start(
+                            out=rows[:, h0 : h0 + STORE_HEADS, j0 : j0 + nj, :], in_=ost[:, h0 : h0 + STORE_HEADS, :, :]
+                        )
 
         nc.vector.memset(wb_raw[:], 0.0)
         nc.vector.memset(one_t[:], 1.0)

@@ -23,7 +23,7 @@ PASSES = THIRDS * J
 EPS = 1e-5
 
 VECTOR_SHARE = 4
-STORE_HEADS = 4
+FIRST_ON_GPSIMD = 2
 
 
 def tile_selfattention_pa_t_kernel(tc, inputs, ln_w, ln_b, w_qkv, out_0, out_1, out_2):
@@ -33,10 +33,10 @@ def tile_selfattention_pa_t_kernel(tc, inputs, ln_w, ln_b, w_qkv, out_0, out_1, 
         keep = ctx.enter_context(tc.tile_pool(name="keep", bufs=1))
         wgp = ctx.enter_context(tc.tile_pool(name="wgp", bufs=2))
         sp = ctx.enter_context(tc.tile_pool(name="sp", bufs=4))
-        xnp = ctx.enter_context(tc.tile_pool(name="xnp", bufs=2 * G))
+        xnp = ctx.enter_context(tc.tile_pool(name="xnp", bufs=3 * G))
         plp = ctx.enter_context(tc.tile_pool(name="plp", bufs=2))
         grp = ctx.enter_context(tc.tile_pool(name="grp", bufs=2))
-        osp = ctx.enter_context(tc.tile_pool(name="osp", bufs=7))
+        osp = ctx.enter_context(tc.tile_pool(name="osp", bufs=6))
         xtp = ctx.enter_context(tc.psum_pool(name="xtp", bufs=1))
         accp = ctx.enter_context(tc.psum_pool(name="accp", bufs=4))
 
@@ -111,17 +111,23 @@ def tile_selfattention_pa_t_kernel(tc, inputs, ln_w, ln_b, w_qkv, out_0, out_1, 
             mv = st[("mv", g)]
             rstd = sp.tile([P, G, 1], F32, name="rstd")
             nc.vector.reciprocal(out=rstd[:], in_=st[("std", g)][:])
+            if g >= FIRST_ON_GPSIMD:
+                nmu = sp.tile([P, G, 1], F32, name="nmu")
+                nc.vector.tensor_scalar_mul(out=nmu[:], in0=mv[:, :, 0:1], scalar1=-1.0)
             for i in range(G):
                 xn = xnp.tile([P, E], F32, name="xn")
                 st[("xn", g, i)] = xn
-                nc.vector.tensor_scalar(
-                    out=xn[:].rearrange("p (u e q) -> p u e q", u=2, e=2),
-                    in0=x_tile(g, i).rearrange("p (u q e) -> p u e q", u=2, e=2),
-                    scalar1=mv[:, i, 0:1],
-                    scalar2=rstd[:, i, 0:1],
-                    op0=ALU.subtract,
-                    op1=ALU.mult,
-                )
+                dst = xn[:].rearrange("p (u e q) -> p u e q", u=2, e=2)
+                src = x_tile(g, i).rearrange("p (u q e) -> p u e q", u=2, e=2)
+                if g >= FIRST_ON_GPSIMD:
+                    nc.gpsimd.tensor_scalar(
+                        out=dst, in0=src, scalar1=nmu[:, i, 0:1], scalar2=rstd[:, i, 0:1], op0=ALU.add, op1=ALU.mult
+                    )
+                else:
+                    nc.vector.tensor_scalar(
+                        out=dst, in0=src, scalar1=mv[:, i, 0:1], scalar2=rstd[:, i, 0:1],
+                        op0=ALU.subtract, op1=ALU.mult,
+                    )
 
         def flip(g):
             xts = [xtp.tile([P, G * P], F32, name="xt%d" % t) for t in range(4)]
@@ -194,11 +200,9 @@ def tile_selfattention_pa_t_kernel(tc, inputs, ln_w, ln_b, w_qkv, out_0, out_1, 
                 else:
                     nc.scalar.copy(out=ost[:, :, j - j0, :], in_=heads)
                 if j == j0 + nj - 1:
-                    rows = outs[t3][b].rearrange("h (p j) d -> p h j d", j=J)
-                    for h0 in range(0, H, STORE_HEADS):
-                        nc.sync.dma_start(
-                            out=rows[:, h0 : h0 + STORE_HEADS, j0 : j0 + nj, :], in_=ost[:, h0 : h0 + STORE_HEADS, :, :]
-                        )
+                    nc.sync.dma_start(
+                        out=outs[t3][b].rearrange("h (p j) d -> p h j d", j=J)[:, :, j0 : j0 + nj, :], in_=ost[:]
+                    )
 
         nc.vector.memset(wb_raw[:], 0.0)
         nc.vector.memset(one_t[:], 1.0)
@@ -223,7 +227,7 @@ def tile_selfattention_pa_t_kernel(tc, inputs, ln_w, ln_b, w_qkv, out_0, out_1, 
         w_quant(0)
         for s in range(1, NG + 3):
             if s <= NG:
-                affine(s - 1, 4 if s <= 2 else 2)
+                affine(s - 1, 4 if s <= 2 else 1)
                 regroup(s - 1)
             if s in (2, 3) or s >= 5:
                 share = VECTOR_SHARE if s <= NG else 2

@@ -22,8 +22,7 @@ THIRDS = 3
 PASSES = THIRDS * J
 EPS = 1e-5
 
-VECTOR_SHARE = 4
-FIRST_ON_GPSIMD = 2
+VECTOR_SHARE = 6
 
 
 def tile_selfattention_pa_t_kernel(tc, inputs, ln_w, ln_b, w_qkv, out_0, out_1, out_2):
@@ -33,10 +32,10 @@ def tile_selfattention_pa_t_kernel(tc, inputs, ln_w, ln_b, w_qkv, out_0, out_1, 
         keep = ctx.enter_context(tc.tile_pool(name="keep", bufs=1))
         wgp = ctx.enter_context(tc.tile_pool(name="wgp", bufs=2))
         sp = ctx.enter_context(tc.tile_pool(name="sp", bufs=4))
-        xnp = ctx.enter_context(tc.tile_pool(name="xnp", bufs=3 * G))
+        xnp = ctx.enter_context(tc.tile_pool(name="xnp", bufs=2 * G))
         plp = ctx.enter_context(tc.tile_pool(name="plp", bufs=2))
         grp = ctx.enter_context(tc.tile_pool(name="grp", bufs=2))
-        osp = ctx.enter_context(tc.tile_pool(name="osp", bufs=6))
+        osp = ctx.enter_context(tc.tile_pool(name="osp", bufs=7))
         xtp = ctx.enter_context(tc.psum_pool(name="xtp", bufs=1))
         accp = ctx.enter_context(tc.psum_pool(name="accp", bufs=4))
 
@@ -111,23 +110,17 @@ def tile_selfattention_pa_t_kernel(tc, inputs, ln_w, ln_b, w_qkv, out_0, out_1, 
             mv = st[("mv", g)]
             rstd = sp.tile([P, G, 1], F32, name="rstd")
             nc.vector.reciprocal(out=rstd[:], in_=st[("std", g)][:])
-            if g >= FIRST_ON_GPSIMD:
-                nmu = sp.tile([P, G, 1], F32, name="nmu")
-                nc.vector.tensor_scalar_mul(out=nmu[:], in0=mv[:, :, 0:1], scalar1=-1.0)
             for i in range(G):
                 xn = xnp.tile([P, E], F32, name="xn")
                 st[("xn", g, i)] = xn
-                dst = xn[:].rearrange("p (u e q) -> p u e q", u=2, e=2)
-                src = x_tile(g, i).rearrange("p (u q e) -> p u e q", u=2, e=2)
-                if g >= FIRST_ON_GPSIMD:
-                    nc.gpsimd.tensor_scalar(
-                        out=dst, in0=src, scalar1=nmu[:, i, 0:1], scalar2=rstd[:, i, 0:1], op0=ALU.add, op1=ALU.mult
-                    )
-                else:
-                    nc.vector.tensor_scalar(
-                        out=dst, in0=src, scalar1=mv[:, i, 0:1], scalar2=rstd[:, i, 0:1],
-                        op0=ALU.subtract, op1=ALU.mult,
-                    )
+                nc.vector.tensor_scalar(
+                    out=xn[:].rearrange("p (u e q) -> p u e q", u=2, e=2),
+                    in0=x_tile(g, i).rearrange("p (u q e) -> p u e q", u=2, e=2),
+                    scalar1=mv[:, i, 0:1],
+                    scalar2=rstd[:, i, 0:1],
+                    op0=ALU.subtract,
+                    op1=ALU.mult,
+                )
 
         def flip(g):
             xts = [xtp.tile([P, G * P], F32, name="xt%d" % t) for t in range(4)]
@@ -227,7 +220,7 @@ def tile_selfattention_pa_t_kernel(tc, inputs, ln_w, ln_b, w_qkv, out_0, out_1, 
         w_quant(0)
         for s in range(1, NG + 3):
             if s <= NG:
-                affine(s - 1, 4 if s <= 2 else 1)
+                affine(s - 1, 4 if s <= 2 else 3)
                 regroup(s - 1)
             if s in (2, 3) or s >= 5:
                 share = VECTOR_SHARE if s <= NG else 2

@@ -17,12 +17,24 @@ P = 128
 NB, SEQ, E, H, DH = 4, 1024, 512, 8, 64
 J = SEQ // P
 G = 4
-NG = NB * J // G
+GROUPS = [(0, 2), (2, 2)] + [(i, G) for i in range(G, NB * J, G)]
+NG = len(GROUPS)
+GROUP_OF = {first + i: (g, i) for g, (first, count) in enumerate(GROUPS) for i in range(count)}
 THIRDS = 3
-PASSES = THIRDS * J
 EPS = 1e-5
 
-VECTOR_SHARE = 6
+
+def pass_order():
+    order = []
+    for b in range(NB):
+        for j0 in range(0, J, G):
+            for t3 in range(THIRDS):
+                for j in range(j0, j0 + G):
+                    order.append((b, t3, j, j0, G) if b <= 2 else (b, t3, j, 0, J))
+    return order
+
+
+ORDER = pass_order()
 
 
 def tile_selfattention_pa_t_kernel(tc, inputs, ln_w, ln_b, w_qkv, out_0, out_1, out_2):
@@ -43,18 +55,20 @@ def tile_selfattention_pa_t_kernel(tc, inputs, ln_w, ln_b, w_qkv, out_0, out_1, 
         one_t = keep.tile([P, 1], F32, name="one_t")
         junk = keep.tile([P, 1], F32, name="junk")
         ident = keep.tile([P, P], F32, name="ident")
+        minus_half = keep.tile([P, G, 1], F32, name="minus_half")
         x_sb = [keep.tile([P, J, E], BF16, name="x%d" % b) for b in range(NB)]
         w_sb = keep.tile([P, THIRDS * 4, E], BF16, name="w_sb")
         wcodes = keep.tile([P, THIRDS * E], U32, name="wcodes", align_bytes=64)
         wscales = keep.tile([P, THIRDS * E], U8, name="wscales", align_bytes=64)
-        xc = [keep.tile([P, G * P], U32, name="xc%d" % g, align_bytes=64) for g in range(NG)]
-        xs = [keep.tile([P, G * P], U8, name="xs%d" % g, align_bytes=64) for g in range(NG)]
+        xc = [keep.tile([P, n * P], U32, name="xc%d" % g, align_bytes=64) for g, (first, n) in enumerate(GROUPS)]
+        xs = [keep.tile([P, n * P], U8, name="xs%d" % g, align_bytes=64) for g, (first, n) in enumerate(GROUPS)]
         wbc = keep.tile([P, 8], F32, name="wbc")
         xv = [inputs[b].rearrange("(p j) k -> p j k", j=J) for b in range(NB)]
         st = {}
 
         def x_tile(g, i):
-            return x_sb[g // 2][:, G * (g % 2) + i, :]
+            tok = GROUPS[g][0] + i
+            return x_sb[tok // J][:, tok % J, :]
 
         def load_w(t):
             nc.sync.dma_start(
@@ -67,18 +81,17 @@ def tile_selfattention_pa_t_kernel(tc, inputs, ln_w, ln_b, w_qkv, out_0, out_1, 
             nc.tensor.transpose(wbT[:, 0:P], wb_raw[:].bitcast(F32), ident[:])
             nc.vector.tensor_copy(out=wbc[:], in_=wbT[:, 0:4].bitcast(BF16))
 
-        def w_flip(t):
-            wg = wgp.tile([P, E, 2], F32, name="wg", align_bytes=64)
-            st[("wg", t)] = wg
-            for half in range(2):
-                wt = accp.tile([P, 2, 2 * P], F32, tag="acc", name="wt")
-                for rr in range(2):
-                    words = w_sb[:, 4 * t + 2 * half + rr, :].bitcast(F32)
-                    for u in range(2):
-                        nc.tensor.transpose(wt[:, u, P * rr : P * rr + P], words[:, P * u : P * u + P], ident[:])
-                nc.scalar.copy(
-                    out=wg[:, 2 * P * half : 2 * P * half + 2 * P, :], in_=wt[:].rearrange("p u n -> p n u")
-                )
+        def w_flip(t, half):
+            if half == 0:
+                st[("wg", t)] = wgp.tile([P, E, 2], F32, name="wg", align_bytes=64)
+            wt = accp.tile([P, 2, 2 * P], F32, tag="acc", name="wt")
+            for rr in range(2):
+                words = w_sb[:, 4 * t + 2 * half + rr, :].bitcast(F32)
+                for u in range(2):
+                    nc.tensor.transpose(wt[:, u, P * rr : P * rr + P], words[:, P * u : P * u + P], ident[:])
+            nc.scalar.copy(
+                out=st[("wg", t)][:, 2 * P * half : 2 * P * half + 2 * P, :], in_=wt[:].rearrange("p u n -> p n u")
+            )
 
         def w_quant(t):
             nc.vector.quantize_mx(
@@ -87,74 +100,95 @@ def tile_selfattention_pa_t_kernel(tc, inputs, ln_w, ln_b, w_qkv, out_0, out_1, 
                 in_=st[("wg", t)][:].rearrange("p n u -> p (n u)").bitcast(BF16),
             )
 
-        def stats(g, first=0, last=G):
-            if first == 0:
+        def stats(g, i):
+            if i == 0:
                 st[("sts", g)] = sp.tile([P, G, 6], F32, name="sts")
-                st[("mv", g)] = sp.tile([P, G, 2], F32, name="mv")
-            sts, mv = st[("sts", g)], st[("mv", g)]
-            for i in range(first, last):
-                nc.vector.bn_stats(out=sts[:, i, :], in_=x_tile(g, i))
-            for i in range(first, last):
-                nc.vector.bn_aggr(out=mv[:, i, :], in_=sts[:, i, :])
-            if last == G:
-                ve = sp.tile([P, G, 1], F32, name="ve")
-                st[("ve", g)] = ve
-                nc.vector.tensor_scalar_add(out=ve[:], in0=mv[:, :, 1:2], scalar1=EPS)
+            nc.vector.bn_stats(out=st[("sts", g)][:, i, :], in_=x_tile(g, i))
 
-        def root(g):
+        def aggregate(g):
+            n = GROUPS[g][1]
+            mv = sp.tile([P, G, 2], F32, name="mv")
+            ve = sp.tile([P, G, 1], F32, name="ve")
             std = sp.tile([P, G, 1], F32, name="std")
-            st[("std", g)] = std
-            nc.scalar.activation(out=std[:], in_=st[("ve", g)][:], func=ACT.Sqrt)
+            st[("mean", g)], st[("std", g)] = mv, std
+            for i in range(n):
+                nc.vector.bn_aggr(out=mv[:, i, :], in_=st[("sts", g)][:, i, :])
+            nc.vector.tensor_scalar_add(out=ve[:, 0:n, :], in0=mv[:, 0:n, 1:2], scalar1=EPS)
+            nc.scalar.activation(out=std[:, 0:n, :], in_=ve[:, 0:n, :], func=ACT.Sqrt)
 
-        def normalise(g):
-            mv = st[("mv", g)]
-            rstd = sp.tile([P, G, 1], F32, name="rstd")
-            nc.vector.reciprocal(out=rstd[:], in_=st[("std", g)][:])
-            for i in range(G):
-                xn = xnp.tile([P, E], F32, name="xn")
-                st[("xn", g, i)] = xn
-                nc.vector.tensor_scalar(
-                    out=xn[:].rearrange("p (u e q) -> p u e q", u=2, e=2),
-                    in0=x_tile(g, i).rearrange("p (u q e) -> p u e q", u=2, e=2),
-                    scalar1=mv[:, i, 0:1],
-                    scalar2=rstd[:, i, 0:1],
-                    op0=ALU.subtract,
-                    op1=ALU.mult,
+        def reciprocal(g):
+            n = GROUPS[g][1]
+            rstd = sp.tile([P, G, 1], F32, tag="rstd", name="rstd")
+            st[("rstd", g)] = rstd
+            nc.vector.reciprocal(out=rstd[:, 0:n, :], in_=st[("std", g)][:, 0:n, :])
+
+        def moments(g):
+            sts = st[("sts", g)]
+            mean = sp.tile([P, G, 1], F32, tag="mean", name="mean")
+            rstd = sp.tile([P, G, 1], F32, tag="rstd", name="rstd")
+            half = sp.tile([P, G, 1], F32, name="half")
+            var = sp.tile([P, G, 1], F32, name="var")
+            st[("mean", g)], st[("rstd", g)] = mean, rstd
+            mean_even, mean_odd = sts[:, :, 1:2], sts[:, :, 4:5]
+            nc.gpsimd.tensor_tensor(out=mean[:], in0=mean_even, in1=mean_odd, op=ALU.add)
+            nc.gpsimd.tensor_tensor(out=var[:], in0=sts[:, :, 2:3], in1=sts[:, :, 5:6], op=ALU.add)
+            nc.gpsimd.tensor_scalar(out=mean[:], in0=mean[:], scalar1=0.5, scalar2=0.0, op0=ALU.mult, op1=ALU.add)
+            nc.gpsimd.tensor_scalar(out=var[:], in0=var[:], scalar1=1.0 / E, scalar2=EPS, op0=ALU.mult, op1=ALU.add)
+            nc.gpsimd.tensor_tensor(out=half[:], in0=mean_even, in1=mean[:], op=ALU.subtract)
+            nc.gpsimd.tensor_tensor(out=half[:], in0=half[:], in1=half[:], op=ALU.mult)
+            nc.gpsimd.tensor_tensor(out=var[:], in0=half[:], in1=var[:], op=ALU.add)
+            nc.gpsimd.tensor_tensor(out=rstd[:], in0=var[:], in1=minus_half[:], op=ALU.pow)
+
+        def normalise(g, i):
+            xn = xnp.tile([P, E], F32, name="xn")
+            st[("xn", g, i)] = xn
+            nc.vector.tensor_scalar(
+                out=xn[:].rearrange("p (u e q) -> p u e q", u=2, e=2),
+                in0=x_tile(g, i).rearrange("p (u q e) -> p u e q", u=2, e=2),
+                scalar1=st[("mean", g)][:, i, 0:1],
+                scalar2=st[("rstd", g)][:, i, 0:1],
+                op0=ALU.subtract,
+                op1=ALU.mult,
+            )
+
+        def flip(g, i):
+            n = GROUPS[g][1]
+            if i == 0:
+                if n == G:
+                    banks = [xtp.tile([P, G * P], F32, name="xt%d" % t) for t in range(4)]
+                    st[("xt", g)] = [banks[t][:] for t in range(4)]
+                else:
+                    banks = [xtp.tile([P, G * P], F32, name="xt%d" % (2 * (g % 2) + u)) for u in range(2)]
+                    st[("xt", g)] = [banks[t // 2][:, n * P * (t % 2) : n * P * (t % 2) + n * P] for t in range(4)]
+            for t in range(4):
+                nc.tensor.transpose(
+                    st[("xt", g)][t][:, P * i : P * i + P], st[("xn", g, i)][:, P * t : P * t + P], ident[:]
                 )
 
-        def flip(g):
-            xts = [xtp.tile([P, G * P], F32, name="xt%d" % t) for t in range(4)]
-            st[("xt", g)] = xts
-            with tc.high_priority():
-                for i in range(G):
-                    for t in range(4):
-                        nc.tensor.transpose(
-                            xts[t][:, P * i : P * i + P], st[("xn", g, i)][:, P * t : P * t + P], ident[:]
-                        )
+        def affine(g, t, on_scalar):
+            if t == 0:
+                st[("pl", g)] = plp.tile([P, 4, GROUPS[g][1] * P], BF16, tag="pl", name="pl")
+            pl, bank = st[("pl", g)], st[("xt", g)][t]
+            if on_scalar:
+                nc.scalar.activation(
+                    out=pl[:, t, :], in_=bank, func=ACT.Identity,
+                    bias=wbc[:, 4 + t : 5 + t], scale=wbc[:, t : t + 1],
+                )
+            else:
+                nc.vector.tensor_scalar(
+                    out=pl[:, t, :], in0=bank,
+                    scalar1=wbc[:, t : t + 1], scalar2=wbc[:, 4 + t : 5 + t], op0=ALU.mult, op1=ALU.add,
+                )
 
-        def affine(g, on_scalar):
-            pl = plp.tile([P, 4, G * P], BF16, name="pl")
-            st[("pl", g)] = pl
-            for t in range(4):
-                bank = st[("xt", g)][t]
-                if t < on_scalar:
-                    nc.scalar.activation(
-                        out=pl[:, t, :], in_=bank[:], func=ACT.Identity,
-                        bias=wbc[:, 4 + t : 5 + t], scale=wbc[:, t : t + 1],
-                    )
-                else:
-                    nc.vector.tensor_scalar(
-                        out=pl[:, t, :], in0=bank[:],
-                        scalar1=wbc[:, t : t + 1], scalar2=wbc[:, 4 + t : 5 + t], op0=ALU.mult, op1=ALU.add,
-                    )
-
-        def regroup(g):
-            gr = grp.tile([P, G * P, 4], BF16, name="gr", align_bytes=64)
+        def regroup(g, on_gpsimd):
+            gr = grp.tile([P, GROUPS[g][1] * P, 4], BF16, tag="gr", name="gr", align_bytes=64)
             st[("gr", g)] = gr
-            nc.vector.tensor_copy(
-                out=gr[:].rearrange("p (c i) t -> p c t i", i=4),
-                in_=st[("pl", g)][:].rearrange("p t (c i) -> p c t i", i=4),
-            )
+            out = gr[:].rearrange("p (c i) t -> p c t i", i=4)
+            in_ = st[("pl", g)][:].rearrange("p t (c i) -> p c t i", i=4)
+            if on_gpsimd:
+                nc.gpsimd.tensor_scalar(out=out, in0=in_, scalar1=1.0, scalar2=0.0, op0=ALU.mult, op1=ALU.add)
+            else:
+                nc.vector.tensor_copy(out=out, in_=in_)
 
         def quant(g):
             nc.vector.quantize_mx(
@@ -163,20 +197,15 @@ def tile_selfattention_pa_t_kernel(tc, inputs, ln_w, ln_b, w_qkv, out_0, out_1, 
 
         done = [0]
 
-        def project(count, on_vector):
-            for i in range(count):
-                b, n = done[0] // PASSES, done[0] % PASSES
+        def project(engines):
+            for engine in engines:
+                b, t3, j, j0, nj = ORDER[done[0]]
                 done[0] += 1
-                if b == 0:
-                    t3, j0, nj = (n % (PASSES // 2)) // G, G * (n // (PASSES // 2)), G
-                    j = j0 + n % G
-                else:
-                    t3, j0, nj = n // J, 0, J
-                    j = n % J
                 if j == j0:
-                    st["ost"] = osp.tile([P, H, nj, DH], F32, tag="ost", name="ost")
-                ost = st["ost"]
-                g, c = 2 * b + j // G, P * (j % G)
+                    st[("ost", t3)] = osp.tile([P, H, nj, DH], F32, tag="ost", name="ost")
+                ost = st[("ost", t3)]
+                g, i_tile = GROUP_OF[J * b + j]
+                c = P * i_tile
                 acc = accp.tile([P, E], F32, tag="acc", name="acc")
                 nc.tensor.matmul_mx(
                     out=acc[:],
@@ -188,7 +217,7 @@ def tile_selfattention_pa_t_kernel(tc, inputs, ln_w, ln_b, w_qkv, out_0, out_1, 
                     stop=True,
                 )
                 heads = acc[:].rearrange("p (h d) -> p h d", h=H)
-                if on_vector(i):
+                if engine == "V":
                     nc.vector.tensor_copy(out=ost[:, :, j - j0, :], in_=heads)
                 else:
                     nc.scalar.copy(out=ost[:, :, j - j0, :], in_=heads)
@@ -197,43 +226,99 @@ def tile_selfattention_pa_t_kernel(tc, inputs, ln_w, ln_b, w_qkv, out_0, out_1, 
                         out=outs[t3][b].rearrange("h (p j) d -> p h j d", j=J)[:, :, j0 : j0 + nj, :], in_=ost[:]
                     )
 
+        def step(g, before, between, after):
+            project(before)
+            if g > 3:
+                quant(g - 1)
+            project(between)
+            for i in range(G):
+                normalise(g, i)
+                flip(g, i)
+            if g + 2 < NG:
+                for i in range(G):
+                    stats(g + 2, i)
+            for t in range(4):
+                affine(g, t, True)
+            regroup(g, True)
+            if g + 2 < NG:
+                moments(g + 2)
+            project(after)
+
         nc.vector.memset(wb_raw[:], 0.0)
         nc.vector.memset(one_t[:], 1.0)
         nc.scalar.activation(out=junk[:], in_=one_t[:], func=ACT.Sqrt)
         make_identity(nc, ident[:])
-        nc.sync.dma_start(out=x_sb[0][:, 0:G, :], in_=xv[0][:, 0:G, :])
+        nc.gpsimd.memset(minus_half[:], -0.5)
+        nc.sync.dma_start(out=x_sb[0][:, 0:2, :], in_=xv[0][:, 0:2, :])
         nc.sync.dma_start(out=wb_raw[0:2, :], in_=ln_w.rearrange("(u c) -> u c", u=2))
         nc.sync.dma_start(out=wb_raw[2:4, :], in_=ln_b.rearrange("(u c) -> u c", u=2))
+        nc.sync.dma_start(out=x_sb[0][:, 2:4, :], in_=xv[0][:, 2:4, :])
         load_w(0)
-        nc.sync.dma_start(out=x_sb[0][:, G:J, :], in_=xv[0][:, G:J, :])
         load_w(1)
+        nc.sync.dma_start(out=x_sb[0][:, 4:J, :], in_=xv[0][:, 4:J, :])
         load_w(2)
         for b in range(1, NB):
             nc.sync.dma_start(out=x_sb[b][:], in_=xv[b])
 
-        gain_bias()
-        stats(0)
-        root(0)
-        normalise(0)
-        flip(0)
-        w_flip(0)
-        w_quant(0)
-        for s in range(1, NG + 3):
-            if s <= NG:
-                affine(s - 1, 4 if s <= 2 else 3)
-                regroup(s - 1)
-            if s in (2, 3) or s >= 5:
-                share = VECTOR_SHARE if s <= NG else 2
-                project(PASSES // 2, lambda i: i % share == share - 1)
-            if s < NG:
-                stats(s)
-                root(s)
-                normalise(s)
-                flip(s)
-            if s <= NG:
-                quant(s - 1)
-            if s == 1:
-                w_flip(1)
-                w_quant(1)
-                w_flip(2)
-                w_quant(2)
+        with tc.manual_schedule():
+            for i in range(2):
+                stats(0, i)
+            aggregate(0)
+            gain_bias()
+            for i in range(2):
+                stats(1, i)
+            aggregate(1)
+            for g in range(2):
+                reciprocal(g)
+                normalise(g, 0)
+                normalise(g, 1)
+                if g == 0:
+                    w_flip(0, 0)
+                    w_flip(0, 1)
+                flip(g, 0)
+                flip(g, 1)
+            for t in range(4):
+                affine(0, t, t < 3)
+            w_quant(0)
+            regroup(0, False)
+            for t in range(4):
+                affine(1, t, t < 3)
+            quant(0)
+            regroup(1, False)
+            w_flip(1, 0)
+            w_flip(1, 1)
+            quant(1)
+            w_quant(1)
+            for i in range(G):
+                stats(2, i)
+            moments(2)
+            project("SSSS")
+            w_flip(2, 0)
+            w_flip(2, 1)
+            project("SSSS")
+            stats(3, 0)
+            stats(3, 1)
+            w_quant(2)
+            project("SSSS")
+            stats(3, 2)
+            for i in range(G):
+                normalise(2, i)
+            for i in range(G):
+                flip(2, i)
+            stats(3, 3)
+            moments(3)
+            for t in range(4):
+                affine(2, t, t < 2)
+            regroup(2, False)
+            stats(4, 0)
+            quant(2)
+            for i in range(1, G):
+                stats(4, i)
+            moments(4)
+
+            step(3, "", "SVSSS", "VSV")
+            for g in range(4, NG):
+                step(g, "SVSS", "S", "VSVSVSS")
+            project("SV" * 2)
+            quant(NG - 1)
+            project(("SV" * len(ORDER))[: len(ORDER) - done[0]])

@@ -180,15 +180,13 @@ def tile_selfattention_pa_t_kernel(tc, inputs, ln_w, ln_b, w_qkv, out_0, out_1, 
                     scalar1=wbc[:, t : t + 1], scalar2=wbc[:, 4 + t : 5 + t], op0=ALU.mult, op1=ALU.add,
                 )
 
-        def regroup(g, on_gpsimd):
+        def regroup(g):
             gr = grp.tile([P, GROUPS[g][1] * P, 4], BF16, tag="gr", name="gr", align_bytes=64)
             st[("gr", g)] = gr
-            out = gr[:].rearrange("p (c i) t -> p c t i", i=4)
-            in_ = st[("pl", g)][:].rearrange("p t (c i) -> p c t i", i=4)
-            if on_gpsimd:
-                nc.gpsimd.tensor_scalar(out=out, in0=in_, scalar1=1.0, scalar2=0.0, op0=ALU.mult, op1=ALU.add)
-            else:
-                nc.vector.tensor_copy(out=out, in_=in_)
+            nc.vector.tensor_copy(
+                out=gr[:].rearrange("p (c i) t -> p c t i", i=4),
+                in_=st[("pl", g)][:].rearrange("p t (c i) -> p c t i", i=4),
+            )
 
         def quant(g):
             nc.vector.quantize_mx(
@@ -226,23 +224,23 @@ def tile_selfattention_pa_t_kernel(tc, inputs, ln_w, ln_b, w_qkv, out_0, out_1, 
                         out=outs[t3][b].rearrange("h (p j) d -> p h j d", j=J)[:, :, j0 : j0 + nj, :], in_=ost[:]
                     )
 
-        def step(g, before, between, after):
-            project(before)
-            if g > 3:
-                quant(g - 1)
-            project(between)
+        def step(g, p):
+            project(p[0])
             for i in range(G):
                 normalise(g, i)
                 flip(g, i)
-            if g + 2 < NG:
+            project(p[1])
+            if g + 1 < NG:
                 for i in range(G):
-                    stats(g + 2, i)
+                    stats(g + 1, i)
+                moments(g + 1)
             for t in range(4):
-                affine(g, t, True)
-            regroup(g, True)
-            if g + 2 < NG:
-                moments(g + 2)
-            project(after)
+                affine(g, t, t < 3)
+            project(p[2])
+            regroup(g)
+            project(p[3])
+            quant(g)
+            project(p[4])
 
         nc.vector.memset(wb_raw[:], 0.0)
         nc.vector.memset(one_t[:], 1.0)
@@ -280,11 +278,11 @@ def tile_selfattention_pa_t_kernel(tc, inputs, ln_w, ln_b, w_qkv, out_0, out_1, 
             for t in range(4):
                 affine(0, t, t < 3)
             w_quant(0)
-            regroup(0, False)
+            regroup(0)
             for t in range(4):
                 affine(1, t, t < 3)
             quant(0)
-            regroup(1, False)
+            regroup(1)
             w_flip(1, 0)
             w_flip(1, 1)
             quant(1)
@@ -309,16 +307,9 @@ def tile_selfattention_pa_t_kernel(tc, inputs, ln_w, ln_b, w_qkv, out_0, out_1, 
             moments(3)
             for t in range(4):
                 affine(2, t, t < 2)
-            regroup(2, False)
-            stats(4, 0)
+            regroup(2)
             quant(2)
-            for i in range(1, G):
-                stats(4, i)
-            moments(4)
 
-            step(3, "", "SVSSS", "VSV")
-            for g in range(4, NG):
-                step(g, "SVSS", "S", "VSVSVSS")
-            project("SV" * 2)
-            quant(NG - 1)
+            for g in range(3, NG):
+                step(g, ("SSSS", "", "SS", "VS", "SVSS"))
             project(("SV" * len(ORDER))[: len(ORDER) - done[0]])

@@ -30,7 +30,7 @@ def pass_order():
         for j0 in range(0, J, G):
             for t3 in range(THIRDS):
                 for j in range(j0, j0 + G):
-                    order.append((b, t3, j, j0, G) if b <= 2 else (b, t3, j, 0, J))
+                    order.append((b, t3, j, j0, G) if b <= 3 else (b, t3, j, 0, J))
     return order
 
 

@@ -55,7 +55,6 @@ def tile_selfattention_pa_t_kernel(tc, inputs, ln_w, ln_b, w_qkv, out_0, out_1, 
         one_t = keep.tile([P, 1], F32, name="one_t")
         junk = keep.tile([P, 1], F32, name="junk")
         ident = keep.tile([P, P], F32, name="ident")
-        minus_half = keep.tile([P, G, 1], F32, name="minus_half")
         x_sb = [keep.tile([P, J, E], BF16, name="x%d" % b) for b in range(NB)]
         w_sb = keep.tile([P, THIRDS * 4, E], BF16, name="w_sb")
         wcodes = keep.tile([P, THIRDS * E], U32, name="wcodes", align_bytes=64)
@@ -109,35 +108,22 @@ def tile_selfattention_pa_t_kernel(tc, inputs, ln_w, ln_b, w_qkv, out_0, out_1, 
             n = GROUPS[g][1]
             mv = sp.tile([P, G, 2], F32, name="mv")
             ve = sp.tile([P, G, 1], F32, name="ve")
-            std = sp.tile([P, G, 1], F32, name="std")
-            st[("mean", g)], st[("std", g)] = mv, std
+            st[("mean", g)], st[("ve", g)] = mv, ve
             for i in range(n):
                 nc.vector.bn_aggr(out=mv[:, i, :], in_=st[("sts", g)][:, i, :])
             nc.vector.tensor_scalar_add(out=ve[:, 0:n, :], in0=mv[:, 0:n, 1:2], scalar1=EPS)
-            nc.scalar.activation(out=std[:, 0:n, :], in_=ve[:, 0:n, :], func=ACT.Sqrt)
+
+        def root(g):
+            n = GROUPS[g][1]
+            std = sp.tile([P, G, 1], F32, name="std")
+            st[("std", g)] = std
+            nc.scalar.activation(out=std[:, 0:n, :], in_=st[("ve", g)][:, 0:n, :], func=ACT.Sqrt)
 
         def reciprocal(g):
             n = GROUPS[g][1]
             rstd = sp.tile([P, G, 1], F32, tag="rstd", name="rstd")
             st[("rstd", g)] = rstd
             nc.vector.reciprocal(out=rstd[:, 0:n, :], in_=st[("std", g)][:, 0:n, :])
-
-        def moments(g):
-            sts = st[("sts", g)]
-            mean = sp.tile([P, G, 1], F32, tag="mean", name="mean")
-            rstd = sp.tile([P, G, 1], F32, tag="rstd", name="rstd")
-            half = sp.tile([P, G, 1], F32, name="half")
-            var = sp.tile([P, G, 1], F32, name="var")
-            st[("mean", g)], st[("rstd", g)] = mean, rstd
-            mean_even, mean_odd = sts[:, :, 1:2], sts[:, :, 4:5]
-            nc.gpsimd.tensor_tensor(out=mean[:], in0=mean_even, in1=mean_odd, op=ALU.add)
-            nc.gpsimd.tensor_tensor(out=var[:], in0=sts[:, :, 2:3], in1=sts[:, :, 5:6], op=ALU.add)
-            nc.gpsimd.tensor_scalar(out=mean[:], in0=mean[:], scalar1=0.5, scalar2=0.0, op0=ALU.mult, op1=ALU.add)
-            nc.gpsimd.tensor_scalar(out=var[:], in0=var[:], scalar1=1.0 / E, scalar2=EPS, op0=ALU.mult, op1=ALU.add)
-            nc.gpsimd.tensor_tensor(out=half[:], in0=mean_even, in1=mean[:], op=ALU.subtract)
-            nc.gpsimd.tensor_tensor(out=half[:], in0=half[:], in1=half[:], op=ALU.mult)
-            nc.gpsimd.tensor_tensor(out=var[:], in0=half[:], in1=var[:], op=ALU.add)
-            nc.gpsimd.tensor_tensor(out=rstd[:], in0=var[:], in1=minus_half[:], op=ALU.pow)
 
         def normalise(g, i):
             xn = xnp.tile([P, E], F32, name="xn")
@@ -226,6 +212,7 @@ def tile_selfattention_pa_t_kernel(tc, inputs, ln_w, ln_b, w_qkv, out_0, out_1, 
 
         def step(g, p):
             project(p[0])
+            reciprocal(g)
             for i in range(G):
                 normalise(g, i)
                 flip(g, i)
@@ -233,9 +220,11 @@ def tile_selfattention_pa_t_kernel(tc, inputs, ln_w, ln_b, w_qkv, out_0, out_1, 
             if g + 1 < NG:
                 for i in range(G):
                     stats(g + 1, i)
-                moments(g + 1)
+                aggregate(g + 1)
             for t in range(4):
                 affine(g, t, t < 3)
+            if g + 1 < NG:
+                root(g + 1)
             project(p[2])
             regroup(g)
             project(p[3])
@@ -246,7 +235,6 @@ def tile_selfattention_pa_t_kernel(tc, inputs, ln_w, ln_b, w_qkv, out_0, out_1, 
         nc.vector.memset(one_t[:], 1.0)
         nc.scalar.activation(out=junk[:], in_=one_t[:], func=ACT.Sqrt)
         make_identity(nc, ident[:])
-        nc.gpsimd.memset(minus_half[:], -0.5)
         nc.sync.dma_start(out=x_sb[0][:, 0:2, :], in_=xv[0][:, 0:2, :])
         nc.sync.dma_start(out=wb_raw[0:2, :], in_=ln_w.rearrange("(u c) -> u c", u=2))
         nc.sync.dma_start(out=wb_raw[2:4, :], in_=ln_b.rearrange("(u c) -> u c", u=2))
@@ -262,10 +250,12 @@ def tile_selfattention_pa_t_kernel(tc, inputs, ln_w, ln_b, w_qkv, out_0, out_1, 
             for i in range(2):
                 stats(0, i)
             aggregate(0)
+            root(0)
             gain_bias()
             for i in range(2):
                 stats(1, i)
             aggregate(1)
+            root(1)
             for g in range(2):
                 reciprocal(g)
                 normalise(g, 0)
@@ -289,24 +279,27 @@ def tile_selfattention_pa_t_kernel(tc, inputs, ln_w, ln_b, w_qkv, out_0, out_1, 
             w_quant(1)
             for i in range(G):
                 stats(2, i)
-            moments(2)
+            aggregate(2)
             project("SSSS")
             w_flip(2, 0)
             w_flip(2, 1)
+            root(2)
             project("SSSS")
             stats(3, 0)
             stats(3, 1)
             w_quant(2)
             project("SSSS")
             stats(3, 2)
+            reciprocal(2)
             for i in range(G):
                 normalise(2, i)
             for i in range(G):
                 flip(2, i)
             stats(3, 3)
-            moments(3)
+            aggregate(3)
             for t in range(4):
                 affine(2, t, t < 2)
+            root(3)
             regroup(2)
             quant(2)
 

@@ -20,17 +20,19 @@ G = 4
 GROUPS = [(0, 2), (2, 2)] + [(i, G) for i in range(G, NB * J, G)]
 NG = len(GROUPS)
 GROUP_OF = {first + i: (g, i) for g, (first, count) in enumerate(GROUPS) for i in range(count)}
+BY_SCALAR = {1: 2}
 THIRDS = 3
 EPS = 1e-5
+WHOLE = ((3, 1), (3, 2))
 
 
 def pass_order():
     order = []
     for b in range(NB):
-        for j0 in range(0, J, G):
+        for half in range(0, J, G):
             for t3 in range(THIRDS):
-                for j in range(j0, j0 + G):
-                    order.append((b, t3, j, j0, G) if b <= 3 else (b, t3, j, 0, J))
+                for j in range(half, half + G):
+                    order.append((b, t3, j, 0, J) if (b, t3) in WHOLE else (b, t3, j, half, G))
     return order
 
 
@@ -53,7 +55,9 @@ def tile_selfattention_pa_t_kernel(tc, inputs, ln_w, ln_b, w_qkv, out_0, out_1, 
 
         wb_raw = keep.tile([P, 2 * P], BF16, name="wb_raw")
         one_t = keep.tile([P, 1], F32, name="one_t")
+        eps_t = keep.tile([P, 1], F32, name="eps_t")
         junk = keep.tile([P, 1], F32, name="junk")
+        waste = keep.tile([P, E], BF16, name="waste")
         ident = keep.tile([P, P], F32, name="ident")
         x_sb = [keep.tile([P, J, E], BF16, name="x%d" % b) for b in range(NB)]
         w_sb = keep.tile([P, THIRDS * 4, E], BF16, name="w_sb")
@@ -72,7 +76,7 @@ def tile_selfattention_pa_t_kernel(tc, inputs, ln_w, ln_b, w_qkv, out_0, out_1, 
         def load_w(t):
             nc.sync.dma_start(
                 out=w_sb[:, 4 * t : 4 * t + 4, :],
-                in_=w_qkv[E * t : E * t + E, :].rearrange("(r p) k -> p r k", p=P),
+                in_=w_qkv[E * t : E * t + E, :].rearrange("(p r) k -> p r k", p=P),
             )
 
         def gain_bias():
@@ -83,13 +87,14 @@ def tile_selfattention_pa_t_kernel(tc, inputs, ln_w, ln_b, w_qkv, out_0, out_1, 
         def w_flip(t, half):
             if half == 0:
                 st[("wg", t)] = wgp.tile([P, E, 2], F32, name="wg", align_bytes=64)
-            wt = accp.tile([P, 2, 2 * P], F32, tag="acc", name="wt")
+            wt = accp.tile([P, 2, 2, P], F32, tag="acc", name="wt")
             for rr in range(2):
                 words = w_sb[:, 4 * t + 2 * half + rr, :].bitcast(F32)
                 for u in range(2):
-                    nc.tensor.transpose(wt[:, u, P * rr : P * rr + P], words[:, P * u : P * u + P], ident[:])
+                    nc.tensor.transpose(wt[:, rr, u, :], words[:, P * u : P * u + P], ident[:])
             nc.scalar.copy(
-                out=st[("wg", t)][:, 2 * P * half : 2 * P * half + 2 * P, :], in_=wt[:].rearrange("p u n -> p n u")
+                out=st[("wg", t)][:].rearrange("q (p r) u -> q p r u", r=4)[:, :, 2 * half : 2 * half + 2, :],
+                in_=wt[:].rearrange("q r u p -> q p r u"),
             )
 
         def w_quant(t):
@@ -99,31 +104,42 @@ def tile_selfattention_pa_t_kernel(tc, inputs, ln_w, ln_b, w_qkv, out_0, out_1, 
                 in_=st[("wg", t)][:].rearrange("p n u -> p (n u)").bitcast(BF16),
             )
 
+        def split(g):
+            n = GROUPS[g][1]
+            return n - BY_SCALAR.get(g, 0), n
+
+        def open_stats(g):
+            for what, width in (("sts", 6), ("mv", 2), ("sum", 1), ("dev", 1), ("rstd", 1)):
+                st[(what, g)] = sp.tile([P, G, width], F32, tag=what, name="small")
+
         def stats(g, i):
-            if i == 0:
-                st[("sts", g)] = sp.tile([P, G, 6], F32, name="sts")
-            nc.vector.bn_stats(out=st[("sts", g)][:, i, :], in_=x_tile(g, i))
+            if i < split(g)[0]:
+                nc.vector.bn_stats(out=st[("sts", g)][:, i, :], in_=x_tile(g, i))
+            else:
+                total, minus, dev = st[("sum", g)], st[("mv", g)], st[("dev", g)]
+                nc.scalar.activation(out=waste[:], in_=x_tile(g, i), func=ACT.Copy, accum_out=total[:, i, :])
+                nc.scalar.activation(out=minus[:, i, 0:1], in_=total[:, i, :], func=ACT.Copy, scale=-1.0 / E)
+                nc.scalar.activation(
+                    out=waste[:], in_=x_tile(g, i), func=ACT.Square, bias=minus[:, i, 0:1], accum_out=dev[:, i, :]
+                )
 
         def aggregate(g):
-            n = GROUPS[g][1]
-            mv = sp.tile([P, G, 2], F32, name="mv")
-            ve = sp.tile([P, G, 1], F32, name="ve")
-            st[("mean", g)], st[("ve", g)] = mv, ve
-            for i in range(n):
-                nc.vector.bn_aggr(out=mv[:, i, :], in_=st[("sts", g)][:, i, :])
-            nc.vector.tensor_scalar_add(out=ve[:, 0:n, :], in0=mv[:, 0:n, 1:2], scalar1=EPS)
+            nv, n = split(g)
+            for i in range(nv):
+                nc.vector.bn_aggr(out=st[("mv", g)][:, i, :], in_=st[("sts", g)][:, i, :])
 
-        def root(g):
-            n = GROUPS[g][1]
-            std = sp.tile([P, G, 1], F32, name="std")
-            st[("std", g)] = std
-            nc.scalar.activation(out=std[:, 0:n, :], in_=st[("ve", g)][:, 0:n, :], func=ACT.Sqrt)
-
-        def reciprocal(g):
-            n = GROUPS[g][1]
-            rstd = sp.tile([P, G, 1], F32, tag="rstd", name="rstd")
-            st[("rstd", g)] = rstd
-            nc.vector.reciprocal(out=rstd[:, 0:n, :], in_=st[("std", g)][:, 0:n, :])
+        def root(g, by_scalar):
+            nv, n = split(g)
+            if by_scalar:
+                nc.scalar.activation(
+                    out=st[("rstd", g)][:, nv:n, :], in_=st[("dev", g)][:, nv:n, :],
+                    func=ACT.Abs_reciprocal_sqrt, scale=1.0 / E, bias=eps_t[:],
+                )
+            else:
+                nc.scalar.activation(
+                    out=st[("rstd", g)][:, 0:nv, :], in_=st[("mv", g)][:, 0:nv, 1:2],
+                    func=ACT.Abs_reciprocal_sqrt, bias=eps_t[:],
+                )
 
         def normalise(g, i):
             xn = xnp.tile([P, E], F32, name="xn")
@@ -131,9 +147,9 @@ def tile_selfattention_pa_t_kernel(tc, inputs, ln_w, ln_b, w_qkv, out_0, out_1, 
             nc.vector.tensor_scalar(
                 out=xn[:].rearrange("p (u e q) -> p u e q", u=2, e=2),
                 in0=x_tile(g, i).rearrange("p (u q e) -> p u e q", u=2, e=2),
-                scalar1=st[("mean", g)][:, i, 0:1],
+                scalar1=st[("mv", g)][:, i, 0:1],
                 scalar2=st[("rstd", g)][:, i, 0:1],
-                op0=ALU.subtract,
+                op0=ALU.subtract if i < split(g)[0] else ALU.add,
                 op1=ALU.mult,
             )
 
@@ -210,21 +226,22 @@ def tile_selfattention_pa_t_kernel(tc, inputs, ln_w, ln_b, w_qkv, out_0, out_1, 
                         out=outs[t3][b].rearrange("h (p j) d -> p h j d", j=J)[:, :, j0 : j0 + nj, :], in_=ost[:]
                     )
 
-        def step(g, p):
+        def step(g, p, on_scalar):
+            more = g + 1 < NG
             project(p[0])
-            reciprocal(g)
             for i in range(G):
                 normalise(g, i)
                 flip(g, i)
             project(p[1])
-            if g + 1 < NG:
+            if more:
+                open_stats(g + 1)
                 for i in range(G):
                     stats(g + 1, i)
                 aggregate(g + 1)
             for t in range(4):
-                affine(g, t, t < 3)
-            if g + 1 < NG:
-                root(g + 1)
+                affine(g, t, t < on_scalar)
+            if more:
+                root(g + 1, False)
             project(p[2])
             regroup(g)
             project(p[3])
@@ -233,7 +250,8 @@ def tile_selfattention_pa_t_kernel(tc, inputs, ln_w, ln_b, w_qkv, out_0, out_1, 
 
         nc.vector.memset(wb_raw[:], 0.0)
         nc.vector.memset(one_t[:], 1.0)
-        nc.scalar.activation(out=junk[:], in_=one_t[:], func=ACT.Sqrt)
+        nc.vector.tensor_scalar(out=eps_t[:], in0=one_t[:], scalar1=EPS, scalar2=None, op0=ALU.mult)
+        nc.scalar.activation(out=junk[:], in_=one_t[:], func=ACT.Abs_reciprocal_sqrt)
         make_identity(nc, ident[:])
         nc.sync.dma_start(out=x_sb[0][:, 0:2, :], in_=xv[0][:, 0:2, :])
         nc.sync.dma_start(out=wb_raw[0:2, :], in_=ln_w.rearrange("(u c) -> u c", u=2))
@@ -247,62 +265,68 @@ def tile_selfattention_pa_t_kernel(tc, inputs, ln_w, ln_b, w_qkv, out_0, out_1, 
             nc.sync.dma_start(out=x_sb[b][:], in_=xv[b])
 
         with tc.manual_schedule():
-            for i in range(2):
-                stats(0, i)
+            for g in (0, 1):
+                open_stats(g)
+            stats(0, 0)
+            stats(0, 1)
             aggregate(0)
-            root(0)
+            stats(1, 0)
+            root(0, False)
             gain_bias()
-            for i in range(2):
-                stats(1, i)
-            aggregate(1)
-            root(1)
-            for g in range(2):
-                reciprocal(g)
-                normalise(g, 0)
-                normalise(g, 1)
-                if g == 0:
-                    w_flip(0, 0)
-                    w_flip(0, 1)
-                flip(g, 0)
-                flip(g, 1)
-            for t in range(4):
-                affine(0, t, t < 3)
-            w_quant(0)
+            stats(1, 1)
+            root(1, True)
+            w_flip(0, 0)
+            w_flip(0, 1)
+            normalise(0, 0)
+            normalise(0, 1)
+            flip(0, 0)
+            flip(0, 1)
+            affine(0, 0, False)
+            affine(0, 1, False)
+            normalise(1, 0)
+            normalise(1, 1)
+            flip(1, 0)
+            flip(1, 1)
+            affine(0, 2, True)
+            affine(0, 3, False)
             regroup(0)
+            w_quant(0)
             for t in range(4):
                 affine(1, t, t < 3)
             quant(0)
             regroup(1)
             w_flip(1, 0)
             w_flip(1, 1)
+            open_stats(2)
+            stats(2, 0)
             quant(1)
             w_quant(1)
-            for i in range(G):
+            project("SSSS")
+            for i in range(1, G):
                 stats(2, i)
             aggregate(2)
-            project("SSSS")
             w_flip(2, 0)
             w_flip(2, 1)
-            root(2)
+            root(2, False)
             project("SSSS")
-            stats(3, 0)
-            stats(3, 1)
-            w_quant(2)
-            project("SSSS")
-            stats(3, 2)
-            reciprocal(2)
             for i in range(G):
                 normalise(2, i)
             for i in range(G):
                 flip(2, i)
-            stats(3, 3)
-            aggregate(3)
+            w_quant(2)
             for t in range(4):
                 affine(2, t, t < 2)
-            root(3)
+            project("SSSS")
             regroup(2)
             quant(2)
+            open_stats(3)
+            for i in range(G):
+                stats(3, i)
+            aggregate(3)
+            project("SSSS")
+            root(3, False)
 
-            for g in range(3, NG):
-                step(g, ("SSSS", "", "SS", "VS", "SVSS"))
+            step(3, ("SSSS", "", "S", "", "SSS"), 3)
+            for g in range(4, NG):
+                step(g, ("SSSS", "", "SS", "VS", "SVSS"), 3)
             project(("SV" * len(ORDER))[: len(ORDER) - done[0]])

@@ -20,10 +20,10 @@ G = 4
 GROUPS = [(0, 2), (2, 2)] + [(i, G) for i in range(G, NB * J, G)]
 NG = len(GROUPS)
 GROUP_OF = {first + i: (g, i) for g, (first, count) in enumerate(GROUPS) for i in range(count)}
-BY_SCALAR = {1: 2}
+BY_SCALAR = {0: 1, 1: 1}
 THIRDS = 3
 EPS = 1e-5
-WHOLE = ((3, 1), (3, 2))
+WHOLE = ()
 
 
 def pass_order():
@@ -84,7 +84,7 @@ def tile_selfattention_pa_t_kernel(tc, inputs, ln_w, ln_b, w_qkv, out_0, out_1, 
             nc.tensor.transpose(wbT[:, 0:P], wb_raw[:].bitcast(F32), ident[:])
             nc.vector.tensor_copy(out=wbc[:], in_=wbT[:, 0:4].bitcast(BF16))
 
-        def w_flip(t, half):
+        def w_turn(t, half):
             if half == 0:
                 st[("wg", t)] = wgp.tile([P, E, 2], F32, name="wg", align_bytes=64)
             wt = accp.tile([P, 2, 2, P], F32, tag="acc", name="wt")
@@ -92,10 +92,18 @@ def tile_selfattention_pa_t_kernel(tc, inputs, ln_w, ln_b, w_qkv, out_0, out_1, 
                 words = w_sb[:, 4 * t + 2 * half + rr, :].bitcast(F32)
                 for u in range(2):
                     nc.tensor.transpose(wt[:, rr, u, :], words[:, P * u : P * u + P], ident[:])
+            st[("wt", t, half)] = wt
+
+        def w_out(t, half):
             nc.scalar.copy(
                 out=st[("wg", t)][:].rearrange("q (p r) u -> q p r u", r=4)[:, :, 2 * half : 2 * half + 2, :],
-                in_=wt[:].rearrange("q r u p -> q p r u"),
+                in_=st[("wt", t, half)][:].rearrange("q r u p -> q p r u"),
             )
+
+        def w_flip(t):
+            for half in range(2):
+                w_turn(t, half)
+                w_out(t, half)
 
         def w_quant(t):
             nc.vector.quantize_mx(
@@ -168,7 +176,7 @@ def tile_selfattention_pa_t_kernel(tc, inputs, ln_w, ln_b, w_qkv, out_0, out_1, 
                 )
 
         def affine(g, t, on_scalar):
-            if t == 0:
+            if ("pl", g) not in st:
                 st[("pl", g)] = plp.tile([P, 4, GROUPS[g][1] * P], BF16, tag="pl", name="pl")
             pl, bank = st[("pl", g)], st[("xt", g)][t]
             if on_scalar:
@@ -269,34 +277,35 @@ def tile_selfattention_pa_t_kernel(tc, inputs, ln_w, ln_b, w_qkv, out_0, out_1, 
                 open_stats(g)
             stats(0, 0)
             stats(0, 1)
-            aggregate(0)
+            root(0, True)
             stats(1, 0)
+            aggregate(0)
             root(0, False)
+            aggregate(1)
             gain_bias()
             stats(1, 1)
+            root(1, False)
             root(1, True)
-            w_flip(0, 0)
-            w_flip(0, 1)
-            normalise(0, 0)
-            normalise(0, 1)
-            flip(0, 0)
-            flip(0, 1)
-            affine(0, 0, False)
-            affine(0, 1, False)
-            normalise(1, 0)
-            normalise(1, 1)
-            flip(1, 0)
-            flip(1, 1)
-            affine(0, 2, True)
-            affine(0, 3, False)
+            w_turn(0, 0)
+            w_turn(0, 1)
+            for g in (0, 1):
+                normalise(g, 0)
+                normalise(g, 1)
+                flip(g, 0)
+                flip(g, 1)
+            for t in (2, 3):
+                affine(0, t, False)
+            for t in (0, 1):
+                affine(0, t, True)
+            w_out(0, 0)
+            w_out(0, 1)
             regroup(0)
-            w_quant(0)
             for t in range(4):
                 affine(1, t, t < 3)
+            w_quant(0)
+            w_flip(1)
             quant(0)
             regroup(1)
-            w_flip(1, 0)
-            w_flip(1, 1)
             open_stats(2)
             stats(2, 0)
             quant(1)
@@ -305,8 +314,7 @@ def tile_selfattention_pa_t_kernel(tc, inputs, ln_w, ln_b, w_qkv, out_0, out_1, 
             for i in range(1, G):
                 stats(2, i)
             aggregate(2)
-            w_flip(2, 0)
-            w_flip(2, 1)
+            w_flip(2)
             root(2, False)
             project("SSSS")
             for i in range(G):

@@ -66,7 +66,7 @@ def tile_selfattention_pa_t_kernel(tc, inputs, ln_w, ln_b, w_qkv, out_0, out_1, 
         xc = [keep.tile([P, n * P], U32, name="xc%d" % g, align_bytes=64) for g, (first, n) in enumerate(GROUPS)]
         xs = [keep.tile([P, n * P], U8, name="xs%d" % g, align_bytes=64) for g, (first, n) in enumerate(GROUPS)]
         wbc = keep.tile([P, 8], F32, name="wbc")
-        xv = [inputs[b].rearrange("(p j) k -> p j k", j=J) for b in range(NB)]
+        xv = [inputs[b].rearrange("(f p i) k -> p f i k", f=2, i=G) for b in range(NB)]
         st = {}
 
         def x_tile(g, i):
@@ -230,9 +230,8 @@ def tile_selfattention_pa_t_kernel(tc, inputs, ln_w, ln_b, w_qkv, out_0, out_1, 
                 else:
                     nc.scalar.copy(out=ost[:, :, j - j0, :], in_=heads)
                 if j == j0 + nj - 1:
-                    nc.sync.dma_start(
-                        out=outs[t3][b].rearrange("h (p j) d -> p h j d", j=J)[:, :, j0 : j0 + nj, :], in_=ost[:]
-                    )
+                    rows = outs[t3][b].rearrange("h (f p i) d -> f p h i d", f=2, i=G)
+                    nc.sync.dma_start(out=rows[j0 // G], in_=ost[:])
 
         def step(g, p, on_scalar):
             more = g + 1 < NG
@@ -261,16 +260,16 @@ def tile_selfattention_pa_t_kernel(tc, inputs, ln_w, ln_b, w_qkv, out_0, out_1, 
         nc.vector.tensor_scalar(out=eps_t[:], in0=one_t[:], scalar1=EPS, scalar2=None, op0=ALU.mult)
         nc.scalar.activation(out=junk[:], in_=one_t[:], func=ACT.Abs_reciprocal_sqrt)
         make_identity(nc, ident[:])
-        nc.sync.dma_start(out=x_sb[0][:, 0:2, :], in_=xv[0][:, 0:2, :])
+        nc.sync.dma_start(out=x_sb[0][:, 0:2, :], in_=xv[0][:, 0, 0:2, :])
         nc.sync.dma_start(out=wb_raw[0:2, :], in_=ln_w.rearrange("(u c) -> u c", u=2))
         nc.sync.dma_start(out=wb_raw[2:4, :], in_=ln_b.rearrange("(u c) -> u c", u=2))
-        nc.sync.dma_start(out=x_sb[0][:, 2:4, :], in_=xv[0][:, 2:4, :])
+        nc.sync.dma_start(out=x_sb[0][:, 2:4, :], in_=xv[0][:, 0, 2:4, :])
         load_w(0)
         load_w(1)
-        nc.sync.dma_start(out=x_sb[0][:, 4:J, :], in_=xv[0][:, 4:J, :])
+        nc.sync.dma_start(out=x_sb[0][:, 4:J, :], in_=xv[0][:, 1, :, :])
         load_w(2)
         for b in range(1, NB):
-            nc.sync.dma_start(out=x_sb[b][:], in_=xv[b])
+            nc.sync.dma_start(out=x_sb[b][:].rearrange("p (f i) k -> p f i k", f=2), in_=xv[b])
 
         with tc.manual_schedule():
             for g in (0, 1):
@@ -331,10 +330,12 @@ def tile_selfattention_pa_t_kernel(tc, inputs, ln_w, ln_b, w_qkv, out_0, out_1, 
             for i in range(G):
                 stats(3, i)
             aggregate(3)
-            project("SSSS")
+            project("SSS")
             root(3, False)
+            project("S")
 
             step(3, ("SSSS", "", "S", "", "SSS"), 3)
-            for g in range(4, NG):
-                step(g, ("SSSS", "", "SS", "VS", "SVSS"), 3)
-            project(("SV" * len(ORDER))[: len(ORDER) - done[0]])
+            step(4, ("SSSSS", "", "SSV", "", "SVSS"), 2)
+        for g in range(5, NG):
+            step(g, ("SSSS", "", "SS", "VS", "SVSS"), 3)
+        project(("SV" * len(ORDER))[: len(ORDER) - done[0]])

from contextlib import ExitStack

import concourse.mybir as mybir
from concourse.masks import make_identity

FLOPS = 2 * 4096 * 1536 * 512

F32 = mybir.dt.float32
BF16 = mybir.dt.bfloat16
U32 = mybir.dt.uint32
U8 = mybir.dt.uint8
FP8X4 = mybir.dt.float8_e4m3fn_x4
ALU = mybir.AluOpType
ACT = mybir.ActivationFunctionType

P = 128
NB, SEQ, E, H, DH = 4, 1024, 512, 8, 64
J = SEQ // P
G = 4
GROUPS = [(0, 2), (2, 2)] + [(i, G) for i in range(G, NB * J, G)]
NG = len(GROUPS)
GROUP_OF = {first + i: (g, i) for g, (first, count) in enumerate(GROUPS) for i in range(count)}
BY_SCALAR = {0: 1, 1: 1}
THIRDS = 3
EPS = 1e-5
WHOLE = ()


def pass_order():
    order = []
    for b in range(NB):
        for half in range(0, J, G):
            for t3 in range(THIRDS):
                for j in range(half, half + G):
                    order.append((b, t3, j, 0, J) if (b, t3) in WHOLE else (b, t3, j, half, G))
    return order


ORDER = pass_order()


def tile_selfattention_pa_t_kernel(tc, inputs, ln_w, ln_b, w_qkv, out_0, out_1, out_2):
    nc = tc.nc
    outs = (out_0, out_1, out_2)
    with ExitStack() as ctx:
        keep = ctx.enter_context(tc.tile_pool(name="keep", bufs=1))
        wgp = ctx.enter_context(tc.tile_pool(name="wgp", bufs=2))
        sp = ctx.enter_context(tc.tile_pool(name="sp", bufs=4))
        xnp = ctx.enter_context(tc.tile_pool(name="xnp", bufs=2 * G))
        plp = ctx.enter_context(tc.tile_pool(name="plp", bufs=2))
        grp = ctx.enter_context(tc.tile_pool(name="grp", bufs=2))
        osp = ctx.enter_context(tc.tile_pool(name="osp", bufs=7))
        xtp = ctx.enter_context(tc.psum_pool(name="xtp", bufs=1))
        accp = ctx.enter_context(tc.psum_pool(name="accp", bufs=4))

        wb_raw = keep.tile([P, 2 * P], BF16, name="wb_raw")
        one_t = keep.tile([P, 1], F32, name="one_t")
        eps_t = keep.tile([P, 1], F32, name="eps_t")
        junk = keep.tile([P, 1], F32, name="junk")
        waste = keep.tile([P, E], BF16, name="waste")
        ident = keep.tile([P, P], F32, name="ident")
        x_sb = [keep.tile([P, J, E], BF16, name="x%d" % b) for b in range(NB)]
        w_sb = keep.tile([P, THIRDS * 4, E], BF16, name="w_sb")
        wcodes = keep.tile([P, THIRDS * E], U32, name="wcodes", align_bytes=64)
        wscales = keep.tile([P, THIRDS * E], U8, name="wscales", align_bytes=64)
        xc = [keep.tile([P, n * P], U32, name="xc%d" % g, align_bytes=64) for g, (first, n) in enumerate(GROUPS)]
        xs = [keep.tile([P, n * P], U8, name="xs%d" % g, align_bytes=64) for g, (first, n) in enumerate(GROUPS)]
        wbc = keep.tile([P, 8], F32, name="wbc")
        xv = [inputs[b].rearrange("(f p i) k -> p f i k", f=2, i=G) for b in range(NB)]
        st = {}

        def x_tile(g, i):
            tok = GROUPS[g][0] + i
            return x_sb[tok // J][:, tok % J, :]

        def load_w(t):
            nc.sync.dma_start(
                out=w_sb[:, 4 * t : 4 * t + 4, :],
                in_=w_qkv[E * t : E * t + E, :].rearrange("(p r) k -> p r k", p=P),
            )

        def gain_bias():
            wbT = accp.tile([P, 512], F32, tag="acc", name="wbT")
            nc.tensor.transpose(wbT[:, 0:P], wb_raw[:].bitcast(F32), ident[:])
            nc.vector.tensor_copy(out=wbc[:], in_=wbT[:, 0:4].bitcast(BF16))

        def w_turn(t, half):
            if half == 0:
                st[("wg", t)] = wgp.tile([P, E, 2], F32, name="wg", align_bytes=64)
            wt = accp.tile([P, 2, 2, P], F32, tag="acc", name="wt")
            for rr in range(2):
                words = w_sb[:, 4 * t + 2 * half + rr, :].bitcast(F32)
                for u in range(2):
                    nc.tensor.transpose(wt[:, rr, u, :], words[:, P * u : P * u + P], ident[:])
            st[("wt", t, half)] = wt

        def w_out(t, half):
            nc.scalar.copy(
                out=st[("wg", t)][:].rearrange("q (p r) u -> q p r u", r=4)[:, :, 2 * half : 2 * half + 2, :],
                in_=st[("wt", t, half)][:].rearrange("q r u p -> q p r u"),
            )

        def w_flip(t):
            for half in range(2):
                w_turn(t, half)
                w_out(t, half)

        def w_quant(t):
            nc.vector.quantize_mx(
                out=wcodes[:, E * t : E * t + E].bitcast(FP8X4),
                scales=wscales[:, E * t : E * t + E],
                in_=st[("wg", t)][:].rearrange("p n u -> p (n u)").bitcast(BF16),
            )

        def split(g):
            n = GROUPS[g][1]
            return n - BY_SCALAR.get(g, 0), n

        def open_stats(g):
            for what, width in (("sts", 6), ("mv", 2), ("sum", 1), ("dev", 1), ("rstd", 1)):
                st[(what, g)] = sp.tile([P, G, width], F32, tag=what, name="small")

        def stats(g, i):
            if i < split(g)[0]:
                nc.vector.bn_stats(out=st[("sts", g)][:, i, :], in_=x_tile(g, i))
            else:
                total, minus, dev = st[("sum", g)], st[("mv", g)], st[("dev", g)]
                nc.scalar.activation(out=waste[:], in_=x_tile(g, i), func=ACT.Copy, accum_out=total[:, i, :])
                nc.scalar.activation(out=minus[:, i, 0:1], in_=total[:, i, :], func=ACT.Copy, scale=-1.0 / E)
                nc.scalar.activation(
                    out=waste[:], in_=x_tile(g, i), func=ACT.Square, bias=minus[:, i, 0:1], accum_out=dev[:, i, :]
                )

        def aggregate(g):
            nv, n = split(g)
            for i in range(nv):
                nc.vector.bn_aggr(out=st[("mv", g)][:, i, :], in_=st[("sts", g)][:, i, :])

        def root(g, by_scalar):
            nv, n = split(g)
            if by_scalar:
                nc.scalar.activation(
                    out=st[("rstd", g)][:, nv:n, :], in_=st[("dev", g)][:, nv:n, :],
                    func=ACT.Abs_reciprocal_sqrt, scale=1.0 / E, bias=eps_t[:],
                )
            else:
                nc.scalar.activation(
                    out=st[("rstd", g)][:, 0:nv, :], in_=st[("mv", g)][:, 0:nv, 1:2],
                    func=ACT.Abs_reciprocal_sqrt, bias=eps_t[:],
                )

        def normalise(g, i):
            xn = xnp.tile([P, E], F32, name="xn")
            st[("xn", g, i)] = xn
            nc.vector.tensor_scalar(
                out=xn[:].rearrange("p (u e q) -> p u e q", u=2, e=2),
                in0=x_tile(g, i).rearrange("p (u q e) -> p u e q", u=2, e=2),
                scalar1=st[("mv", g)][:, i, 0:1],
                scalar2=st[("rstd", g)][:, i, 0:1],
                op0=ALU.subtract if i < split(g)[0] else ALU.add,
                op1=ALU.mult,
            )

        def flip(g, i):
            n = GROUPS[g][1]
            if i == 0:
                if n == G:
                    banks = [xtp.tile([P, G * P], F32, name="xt%d" % t) for t in range(4)]
                    st[("xt", g)] = [banks[t][:] for t in range(4)]
                else:
                    banks = [xtp.tile([P, G * P], F32, name="xt%d" % (2 * (g % 2) + u)) for u in range(2)]
                    st[("xt", g)] = [banks[t // 2][:, n * P * (t % 2) : n * P * (t % 2) + n * P] for t in range(4)]
            for t in range(4):
                nc.tensor.transpose(
                    st[("xt", g)][t][:, P * i : P * i + P], st[("xn", g, i)][:, P * t : P * t + P], ident[:]
                )

        def affine(g, t, on_scalar):
            if ("pl", g) not in st:
                st[("pl", g)] = plp.tile([P, 4, GROUPS[g][1] * P], BF16, tag="pl", name="pl")
            pl, bank = st[("pl", g)], st[("xt", g)][t]
            if on_scalar:
                nc.scalar.activation(
                    out=pl[:, t, :], in_=bank, func=ACT.Identity,
                    bias=wbc[:, 4 + t : 5 + t], scale=wbc[:, t : t + 1],
                )
            else:
                nc.vector.tensor_scalar(
                    out=pl[:, t, :], in0=bank,
                    scalar1=wbc[:, t : t + 1], scalar2=wbc[:, 4 + t : 5 + t], op0=ALU.mult, op1=ALU.add,
                )

        def regroup(g):
            gr = grp.tile([P, GROUPS[g][1] * P, 4], BF16, tag="gr", name="gr", align_bytes=64)
            st[("gr", g)] = gr
            nc.vector.tensor_copy(
                out=gr[:].rearrange("p (c i) t -> p c t i", i=4),
                in_=st[("pl", g)][:].rearrange("p t (c i) -> p c t i", i=4),
            )

        def quant(g):
            nc.vector.quantize_mx(
                out=xc[g][:].bitcast(FP8X4), scales=xs[g][:], in_=st[("gr", g)][:].rearrange("p c t -> p (c t)")
            )

        done = [0]

        def project(engines):
            for engine in engines:
                b, t3, j, j0, nj = ORDER[done[0]]
                done[0] += 1
                if j == j0:
                    st[("ost", t3)] = osp.tile([P, H, nj, DH], F32, tag="ost", name="ost")
                ost = st[("ost", t3)]
                g, i_tile = GROUP_OF[J * b + j]
                c = P * i_tile
                acc = accp.tile([P, E], F32, tag="acc", name="acc")
                nc.tensor.matmul_mx(
                    out=acc[:],
                    lhsT=xc[g][:, c : c + P].bitcast(FP8X4),
                    lhsT_scale=xs[g][:, c : c + P],
                    rhs=wcodes[:, E * t3 : E * t3 + E].bitcast(FP8X4),
                    rhs_scale=wscales[:, E * t3 : E * t3 + E],
                    start=True,
                    stop=True,
                )
                heads = acc[:].rearrange("p (h d) -> p h d", h=H)
                if engine == "V":
                    nc.vector.tensor_copy(out=ost[:, :, j - j0, :], in_=heads)
                else:
                    nc.scalar.copy(out=ost[:, :, j - j0, :], in_=heads)
                if j == j0 + nj - 1:
                    rows = outs[t3][b].rearrange("h (f p i) d -> f p h i d", f=2, i=G)
                    nc.sync.dma_start(out=rows[j0 // G], in_=ost[:])

        def step(g, p, on_scalar):
            more = g + 1 < NG
            project(p[0])
            for i in range(G):
                normalise(g, i)
                flip(g, i)
            project(p[1])
            if more:
                open_stats(g + 1)
                for i in range(G):
                    stats(g + 1, i)
                aggregate(g + 1)
            for t in range(4):
                affine(g, t, t < on_scalar)
            if more:
                root(g + 1, False)
            project(p[2])
            regroup(g)
            project(p[3])
            quant(g)
            project(p[4])

        nc.vector.memset(wb_raw[:], 0.0)
        nc.vector.memset(one_t[:], 1.0)
        nc.vector.tensor_scalar(out=eps_t[:], in0=one_t[:], scalar1=EPS, scalar2=None, op0=ALU.mult)
        nc.scalar.activation(out=junk[:], in_=one_t[:], func=ACT.Abs_reciprocal_sqrt)
        make_identity(nc, ident[:])
        nc.sync.dma_start(out=x_sb[0][:, 0:2, :], in_=xv[0][:, 0, 0:2, :])
        nc.sync.dma_start(out=wb_raw[0:2, :], in_=ln_w.rearrange("(u c) -> u c", u=2))
        nc.sync.dma_start(out=wb_raw[2:4, :], in_=ln_b.rearrange("(u c) -> u c", u=2))
        nc.sync.dma_start(out=x_sb[0][:, 2:4, :], in_=xv[0][:, 0, 2:4, :])
        load_w(0)
        load_w(1)
        nc.sync.dma_start(out=x_sb[0][:, 4:J, :], in_=xv[0][:, 1, :, :])
        load_w(2)
        for b in range(1, NB):
            nc.sync.dma_start(out=x_sb[b][:].rearrange("p (f i) k -> p f i k", f=2), in_=xv[b])

        with tc.manual_schedule():
            for g in (0, 1):
                open_stats(g)
            stats(0, 0)
            stats(0, 1)
            root(0, True)
            stats(1, 0)
            aggregate(0)
            root(0, False)
            aggregate(1)
            gain_bias()
            stats(1, 1)
            root(1, False)
            root(1, True)
            w_turn(0, 0)
            w_turn(0, 1)
            for g in (0, 1):
                normalise(g, 0)
                normalise(g, 1)
                flip(g, 0)
                flip(g, 1)
            for t in (2, 3):
                affine(0, t, False)
            for t in (0, 1):
                affine(0, t, True)
            w_out(0, 0)
            w_out(0, 1)
            regroup(0)
            for t in range(4):
                affine(1, t, t < 3)
            w_quant(0)
            w_flip(1)
            quant(0)
            regroup(1)
            open_stats(2)
            stats(2, 0)
            quant(1)
            w_quant(1)
            project("SSSS")
            for i in range(1, G):
                stats(2, i)
            aggregate(2)
            w_flip(2)
            root(2, False)
            project("SSSS")
            for i in range(G):
                normalise(2, i)
            for i in range(G):
                flip(2, i)
            w_quant(2)
            for t in range(4):
                affine(2, t, t < 2)
            project("SSSS")
            regroup(2)
            quant(2)
            open_stats(3)
            for i in range(G):
                stats(3, i)
            aggregate(3)
            project("SSS")
            root(3, False)
            project("S")

            step(3, ("SSSS", "", "S", "", "SSS"), 3)
            step(4, ("SSSSS", "", "SSV", "", "SVSS"), 2)
        for g in range(5, NG):
            step(g, ("SSSS", "", "SS", "VS", "SVSS"), 3)
        project(("SV" * len(ORDER))[: len(ORDER) - done[0]])
